import numpy as np
import ml_dtypes


def mxq(x, axis, fmt="e4m3"):
    dtype, down = {"e4m3": (ml_dtypes.float8_e4m3fn, 7), "e5m2": (ml_dtypes.float8_e5m2, 14)}[fmt]
    v = np.moveaxis(np.asarray(x, np.float32).astype(ml_dtypes.bfloat16).astype(np.float64), axis, -1)
    blocks = v.reshape(v.shape[:-1] + (-1, 32))
    amax = np.abs(blocks).max(-1, keepdims=True)
    byte = np.maximum(np.where(amax > 0, np.frexp(amax)[1] - 1 + 127, 0) - down, 1)
    scale = np.exp2(byte - 127.0)
    codes = (blocks / scale).astype(np.float32).astype(dtype).astype(np.float64)
    return np.moveaxis((codes * scale).reshape(v.shape), -1, axis)


WIDE = False


def mx_kscale(k):
    if not WIDE:
        return np.ones(k)
    levels = np.array([18, -18])
    if k % 512:
        return np.exp2(np.random.permutation(np.resize(levels, k // 32))).repeat(32)
    a = np.empty((k // 512, 16))
    for p in range(k // 512):
        a[p, :8] = np.random.permutation(np.resize(levels, 8))
        for g in range(8):
            far = levels[np.abs(levels - a[p, g]) >= 10]
            a[p, g + 8] = far[np.random.randint(len(far))]
    return np.exp2(a.ravel()).repeat(32)


BF16 = ml_dtypes.bfloat16


def bf(x):
    return np.asarray(x, np.float32).astype(BF16)


def f64(x):
    return np.asarray(x).astype(np.float64)


B, T, C, HQ, HKV, HD = 4, 256, 1024, 16, 4, 128
EPS = 1e-6


def apply_rope(u, cos, sin):
    c = cos[None, :, None, :]
    s = sin[None, :, None, :]
    u1, u2 = u[..., ::2], u[..., 1::2]
    return np.concatenate([u1 * c - u2 * s, u1 * s + u2 * c], axis=-1)


def rmsnorm(u, w):
    return w * (u / np.sqrt(np.mean(u * u, axis=-1, keepdims=True) + EPS))


def head_factors(heads):
    h = np.arange(heads)
    return mx_kscale(heads * HD).reshape(heads, HD)[h, 32 * (h % (HD // 32))]


def setup_inputs():
    s = mx_kscale(B * T).reshape(B, T)
    uq = head_factors(HQ)
    uk = head_factors(HKV)
    inv_freq = 1.0 / (10000.0 ** (np.arange(0, HD, 2) / HD))
    freqs = np.arange(T)[:, None] * inv_freq[None, :]
    x0 = bf(np.random.standard_normal((B, T, C)))
    Wq0 = bf(np.random.standard_normal((HQ * HD, C)) / np.sqrt(C))
    bq = bf(np.random.standard_normal(HQ * HD) * 0.3)
    Wk0 = bf(np.random.standard_normal((HKV * HD, C)) / np.sqrt(C))
    bk = bf(np.random.standard_normal(HKV * HD) * 0.3)
    qn_w = bf(1.0 + 0.1 * np.random.standard_normal(HD))
    kn_w = bf(1.0 + 0.1 * np.random.standard_normal(HD))
    cos = bf(np.cos(freqs))
    sin = bf(np.sin(freqs))
    g0 = np.random.standard_normal((B, T, HQ, HD)) * np.exp2(np.random.randint(-6, 1, (B, T, 1, 1))) * 2.0
    g1 = np.random.standard_normal((B, T, HKV, HD)) * np.exp2(np.random.randint(-6, 1, (B, T, 1, 1))) * 2.0
    q0 = (f64(x0) @ f64(Wq0).T + f64(bq)).reshape(B, T, HQ, HD)
    k0 = (f64(x0) @ f64(Wk0).T + f64(bk)).reshape(B, T, HKV, HD)
    rq = apply_rope(q0, f64(cos), f64(sin))
    rk = apply_rope(k0, f64(cos), f64(sin))
    return {"x": bf(f64(x0) * s[:, :, None]),
            "Wq": bf(f64(Wq0) / np.repeat(uq, HD)[:, None]),
            "bq": bq,
            "Wk": bf(f64(Wk0) / np.repeat(uk, HD)[:, None]),
            "bk": bk,
            "qn_w": qn_w,
            "kn_w": kn_w,
            "cos": cos,
            "sin": sin,
            "rq": np.asarray(rq, np.float32),
            "rk": np.asarray(rk, np.float32),
            "grad_0": bf(g0 / s[:, :, None, None] * uq[None, None, :, None]),
            "grad_1": bf(g1 / s[:, :, None, None] * uk[None, None, :, None])}


def rmsnorm_backward(g, r, w):
    inv = 1.0 / np.sqrt(np.mean(r * r, axis=-1, keepdims=True) + EPS)
    a = g * w
    return inv * (a - r * (inv * inv * np.mean(a * r, axis=-1, keepdims=True)))


def rope_backward(d, cos, sin):
    c = cos[None, :, None, :]
    s = sin[None, :, None, :]
    d1, d2 = d[..., :HD // 2], d[..., HD // 2:]
    return np.stack([d1 * c + d2 * s, d2 * c - d1 * s], axis=-1).reshape(d.shape)


def reference(x, Wq, bq, Wk, bk, qn_w, kn_w, cos, sin, rq, rk, grad_0, grad_1):
    c, s = f64(cos), f64(sin)
    dq = rope_backward(rmsnorm_backward(f64(grad_0), f64(rq), f64(qn_w)), c, s).reshape(B * T, HQ * HD)
    dk = rope_backward(rmsnorm_backward(f64(grad_1), f64(rk), f64(kn_w)), c, s).reshape(B * T, HKV * HD)
    dz = np.concatenate([dq, dk], axis=1)
    w = np.concatenate([f64(Wq), f64(Wk)], axis=0)
    dx = (mxq(dz, 1, "e5m2") @ mxq(w, 0, "e4m3")).reshape(B, T, C)
    xt = mxq(f64(x).reshape(B * T, C), 0, "e4m3")
    dw = mxq(dz, 0, "e5m2").T @ xt
    return dx, dw[:HQ * HD], dw[HQ * HD:]

@@ -1,0 +1,407 @@
+from contextlib import ExitStack
+
+import concourse.mybir as mybir
+from concourse.masks import make_identity
+
+P = 128
+TOKENS, C, HD = 1024, 1024, 128
+FQ, FK = 2048, 512
+EPS = 1e-6
+J = 4
+NH = 4
+GROUPS, QUADS = 2, 5
+UNITS = GROUPS * QUADS
+SPLIT = (4, 3)
+ITEM_LAG = 3
+W = 512
+FLOPS = 2 * 2 * TOKENS * (FQ + FK) * C
+BYTES = TOKENS * C * 2 + (FQ + FK) * C * 2 + TOKENS * (FQ + FK) * 6 + (TOKENS + FQ + FK) * C * 4
+
+F32 = mybir.dt.float32
+BF16 = mybir.dt.bfloat16
+U32 = mybir.dt.uint32
+U8 = mybir.dt.uint8
+E4 = mybir.dt.float8_e4m3fn_x4
+E5 = mybir.dt.float8_e5m2_x4
+ALU = mybir.AluOpType
+ACT = mybir.ActivationFunctionType
+
+
+def tile_gqaselfattention_pa_v_kernel(tc, x, wq, bq, wk, bk, qn_w, kn_w, cos, sin, rq, rk, grad_0, grad_1, out_0, out_1, out_2):
+    nc = tc.nc
+    rq_v = rq.rearrange("b t h d -> (b t) (h d)").rearrange("(g p j) f -> g p j f", p=P, j=J)
+    rk_v = rk.rearrange("b t h d -> (b t) (h d)").rearrange("(g p j) f -> g p j f", p=P, j=J)
+    gq_v = grad_0.rearrange("b t h d -> (b t) (h d)").rearrange("(g p j) f -> g p j f", p=P, j=J)
+    gk_v = grad_1.rearrange("b t h d -> (b t) (h d)").rearrange("(g p j) f -> g p j f", p=P, j=J)
+    x_v = x.rearrange("b t c -> (b t) c").rearrange("(g p j) c -> g p j c", p=P, j=J)
+    wq_v = wq.rearrange("(q p j) c -> q p j c", p=P, j=J)
+    wk_v = wk.rearrange("(q p j) c -> q p j c", p=P, j=J)
+    o0_v = out_0.rearrange("b t c -> (b t) c").rearrange("(g m j) c -> g j m c", m=P, j=J)
+    o1_v = out_1.rearrange("(q m t) c -> q t m c", m=P, t=4)
+    o2_v = out_2.rearrange("(q m t) c -> q t m c", m=P, t=4)
+
+    with ExitStack() as ctx:
+        const = ctx.enter_context(tc.tile_pool(name="const", bufs=1))
+        work = ctx.enter_context(tc.tile_pool(name="work", bufs=2))
+        psum = ctx.enter_context(tc.psum_pool(name="psum", bufs=2))
+        ctx.enter_context(tc.manual_schedule())
+
+        r_t, g_t, gt_t, a_t, ssq_t, std_t, inv_t, nq_t = {}, {}, {}, {}, {}, {}, {}, {}
+        dot_t, nk_t, d0_t, m_t, dzt_t, dzf_t = {}, {}, {}, {}, {}, {}
+        tokq, featq, trp = {}, {}, {}
+        itemq, raw_t, grp_t = {}, {}, {}
+        ostage, part_t = {}, {}
+
+        def scalar_sums(i):
+            return i < 28
+
+        def per_slot(i):
+            return 1 if i < 27 else 2 + i % 2
+
+        def piece_engine(piece):
+            return "S" if piece % 2 == 0 and piece < 8 else "G"
+
+        def load_unit(n):
+            q, g = divmod(n, GROUPS)
+            gg = work.tile([P, J, W], BF16, tag="g", bufs=3)
+            src_g = gk_v[g] if q == 4 else gq_v[g, :, :, W * q : W * (q + 1)]
+            nc.sync.dma_start(out=gg[:], in_=src_g)
+            g_t[n] = gg
+
+        def load_saved(n):
+            q, g = divmod(n, GROUPS)
+            rr = work.tile([P, J, W], F32, tag="r", bufs=3)
+            src_r = rk_v[g] if q == 4 else rq_v[g, :, :, W * q : W * (q + 1)]
+            if n == 0:
+                for j in range(J):
+                    nc.sync.dma_start(out=rr[:, j, :], in_=src_r[:, j, :])
+            else:
+                nc.sync.dma_start(out=rr[:], in_=src_r)
+            r_t[n] = rr
+
+        def r_perm(n, j, h):
+            return r_t[n][:, j, HD * h : HD * (h + 1)].rearrange("p (x b) -> p b x", b=2)
+
+        def ssq(i):
+            n, j = divmod(i, J)
+            if j == 0:
+                ssq_t[n] = work.tile([P, J * NH], F32, tag="ssq", name="ssq_n")
+            for h in range(NH):
+                k = NH * j + h
+                if n == 0 and j % 2 == 1:
+                    junk = work.tile([P, HD], F32, tag="junk_v", bufs=2)
+                    rv = r_t[n][:, j, HD * h : HD * (h + 1)]
+                    nc.vector.scalar_tensor_tensor(out=junk[:], in0=rv, scalar=1.0, in1=rv, op0=ALU.mult, op1=ALU.mult,
+                                                   accum_out=ssq_t[n][:, k : k + 1])
+                    continue
+                junk = work.tile([P, HD], BF16, tag="junk_s", bufs=2)
+                nc.scalar.activation(out=junk[:], in_=r_t[n][:, j, HD * h : HD * (h + 1)], func=ACT.Square,
+                                     accum_out=ssq_t[n][:, k : k + 1])
+
+        def root_mean_sq(n):
+            std = work.tile([P, J * NH], F32, tag="std")
+            nc.scalar.activation(out=std[:], in_=ssq_t[n][:], func=ACT.Sqrt, scale=1.0 / HD, bias=eps_t[:])
+            std_t[n] = std
+
+        def inverse(n):
+            inv = work.tile([P, J * NH], F32, tag="inv")
+            nc.vector.reciprocal(out=inv[:], in_=std_t[n][:])
+            inv_t[n] = inv
+            nq = work.tile([P, J * NH], F32, tag="nq")
+            nc.scalar.activation(out=nq[:], in_=inv[:], func=ACT.Square, scale=HD ** -0.5)
+            nq_t[n] = nq
+
+        def g_transposes(n, half):
+            if half == 0:
+                gt_t[n] = work.tile([P, J * NH, P], BF16, tag="gt", name="gt_n")
+            tp = psum.tile([P, 8, P], BF16, tag="tr")
+            for k in range(8):
+                j, h = divmod(8 * half + k, NH)
+                nc.tensor.transpose(tp[:, k, :], g_t[n][:, j, HD * h : HD * (h + 1)], ident_b[:])
+            nc.scalar.copy(out=gt_t[n][:, 8 * half : 8 * (half + 1), :], in_=tp[:])
+
+        def scaled_grad(i):
+            n, j = divmod(i, J)
+            a = psum.tile([P, NH, HD], F32, tag="a")
+            diag = diag_k if n // GROUPS == 4 else diag_q
+            for h in range(NH):
+                nc.tensor.matmul(a[:, h, :], gt_t[n][:, NH * j + h, :], diag[:], start=True, stop=True)
+            a_t[i] = a
+
+        def a_perm(i, h):
+            return a_t[i][:, h, :].rearrange("p (b x) -> p b x", b=2)
+
+        def dots(i):
+            n, j = divmod(i, J)
+            nk = work.tile([P, NH], F32, tag="nk", bufs=3)
+            nk_t[i] = nk
+            if scalar_sums(i):
+                pr = work.tile([P, NH, HD], F32, tag="prod")
+                nc.vector.tensor_tensor(out=pr[:].rearrange("p h (b x) -> p h b x", b=2),
+                                        in0=a_t[i][:].rearrange("p h (b x) -> p h b x", b=2),
+                                        in1=r_t[n][:, j, :].rearrange("p (h x b) -> p h b x", h=NH, b=2), op=ALU.mult)
+                dot_t[i] = pr
+                return
+            for h in range(NH):
+                k = NH * j + h
+                junk = work.tile([P, HD], F32, tag="junk_v", bufs=2)
+                nc.vector.scalar_tensor_tensor(
+                    out=junk[:].rearrange("p (b x) -> p b x", b=2), in0=a_perm(i, h), scalar=nq_t[n][:, k : k + 1],
+                    in1=r_perm(n, j, h), op0=ALU.mult, op1=ALU.mult, accum_out=nk[:, h : h + 1])
+
+        def sums(i):
+            if not scalar_sums(i):
+                return
+            n, j = divmod(i, J)
+            for h in range(NH):
+                k = NH * j + h
+                junk = work.tile([P, HD], BF16, tag="junk_s", bufs=2)
+                nc.scalar.activation(out=junk[:], in_=dot_t[i][:, h, :], func=ACT.Copy, scale=nq_t[n][:, k : k + 1],
+                                     accum_out=nk_t[i][:, h : h + 1])
+
+        def project(i):
+            n, j = divmod(i, J)
+            d0 = work.tile([P, NH, HD], F32, tag="d0")
+            for h in range(NH):
+                nc.vector.scalar_tensor_tensor(
+                    out=d0[:, h, :].rearrange("p (b x) -> p b x", b=2), in0=r_perm(n, j, h), scalar=nk_t[i][:, h : h + 1],
+                    in1=a_perm(i, h), op0=ALU.mult, op1=ALU.subtract)
+            d0_t[i] = d0
+
+        def rope_products(i):
+            n, j = divmod(i, J)
+            if j == 0:
+                m_t[n] = work.tile([P, J, 8, NH, 32], F32, tag="m", name="m_n")
+            for h in range(NH):
+                k = NH * j + h
+                d = d0_t[i][:, h : h + 1, :].to_broadcast([P, 2, HD]).rearrange("p c (q i) -> p c q i", i=32)
+                tb = tabs[j // 2][:, 256 * (j % 2) : 256 * (j % 2 + 1)].rearrange("p (c q i) -> p c q i", c=2, i=32)
+                nc.vector.scalar_tensor_tensor(
+                    out=m_t[n][:, j, :, h, :].rearrange("p (c q) i -> p c q i", c=2), in0=d, scalar=inv_t[n][:, k : k + 1],
+                    in1=tb, op0=ALU.mult, op1=ALU.mult)
+
+        def add_halves(n, par, ib, eng):
+            if par == 0 and ib == 0:
+                dzt_t[n] = work.tile([P, 4, P, J], BF16, tag="dzt", align_bytes=64, name="dzt_n")
+            mv = m_t[n][:].rearrange("p j (c b f) h i -> p c b f (h i) j", c=2, b=2)
+            eng.tensor_tensor(out=dzt_t[n][:, 2 * ib + par], in0=mv[:, 0, ib, par], in1=mv[:, 1, ib, 1 - par], op=ALU.add)
+
+        def quant_tokens(n):
+            codes = work.tile([P, 4 * P], U32, tag="tokc", bufs=4, align_bytes=64)
+            scales = work.tile([P, 4 * P], U8, tag="toks", bufs=4, align_bytes=64)
+            nc.vector.quantize_mx(out=codes[:].bitcast(E5), scales=scales[:], in_=dzt_t[n][:].rearrange("p t x j -> p (t x j)"))
+            tokq[n] = (codes, scales)
+
+        def dz_transposes(n):
+            words = dzt_t[n][:].rearrange("p t x j -> p (t x j)").bitcast(F32).rearrange("p (t x u) -> p t x u", t=4, u=2)
+            for u in range(2):
+                tp = psum.tile([P, 4, P], F32, tag="tr")
+                for t in range(4):
+                    nc.tensor.transpose(tp[:, t, :], words[:, t, :, u], ident_f[:])
+                trp[n, u] = tp
+
+        def dz_evacuate(n, u, copy):
+            if u == 0:
+                dzf_t[n] = work.tile([P, 4 * P, 4], BF16, tag="dzf", align_bytes=64, name="dzf_n")
+            pv = trp[n, u][:].rearrange("p t x -> p (t x)").bitcast(BF16).rearrange("p (t x e) -> p e x t", t=4, e=2)
+            copy(out=dzf_t[n][:, 2 * P * u : 2 * P * (u + 1), :].rearrange("p (e x) t -> p e x t", e=2), in_=pv)
+
+        def quant_features(n):
+            codes = const.tile([P, 4 * P], U32, align_bytes=64, name="featc%d" % n)
+            scales = const.tile([P, 4 * P], U8, align_bytes=64, name="feats%d" % n)
+            nc.vector.quantize_mx(out=codes[:].bitcast(E5), scales=scales[:], in_=dzf_t[n][:].rearrange("p x t -> p (x t)"))
+            featq[n] = (codes, scales)
+
+        def load_item(k):
+            raw = work.tile([P, J, C], BF16, tag="raw", align_bytes=64)
+            src = x_v[k] if k < 2 else (wk_v[0] if k == 6 else wq_v[k - 2])
+            nc.sync.dma_start(out=raw[:], in_=src)
+            raw_t[k] = raw
+
+        def interleave(piece, eng):
+            k, s = divmod(piece, 4)
+            if s == 0:
+                grp_t[k] = work.tile([P, C, J], BF16, tag="grp", align_bytes=64, name="grp_k")
+            c0 = 256 * s
+            if eng == "S":
+                nc.scalar.copy(out=grp_t[k][:, c0 : c0 + 256, :].rearrange("p (c i) t -> p c t i", i=4),
+                               in_=raw_t[k][:, :, c0 : c0 + 256].rearrange("p t (c i) -> p c t i", i=4))
+            else:
+                nc.gpsimd.tensor_scalar(out=grp_t[k][:, c0 : c0 + 256, :], in0=raw_t[k][:, :, c0 : c0 + 256].rearrange("p t c -> p c t"),
+                                        scalar1=1.0, scalar2=0.0, op0=ALU.mult, op1=ALU.add)
+
+        def quant_item(k):
+            codes = const.tile([P, C], U32, align_bytes=64, name="itemc%d" % k)
+            scales = const.tile([P, C], U8, align_bytes=64, name="items%d" % k)
+            nc.vector.quantize_mx(out=codes[:].bitcast(E4), scales=scales[:], in_=grp_t[k][:].rearrange("p c t -> p (c t)"))
+            itemq[k] = (codes, scales)
+
+        def mx_group(job, tag, copy):
+            kind, q, m, nh = job
+            acc = psum.tile([P, 512], F32, tag=tag, name="acc")
+            ncol = slice(512 * nh, 512 * (nh + 1))
+            mcol = slice(P * m, P * (m + 1))
+            if kind == "dw":
+                passes = [(tokq[GROUPS * q + g], itemq[g]) for g in range(GROUPS)]
+            else:
+                ks = range(SPLIT[q]) if kind == "dxa" else range(SPLIT[q], QUADS)
+                passes = [(featq[GROUPS * k + q], itemq[2 + k]) for k in ks]
+            for s, (lhs, rhs) in enumerate(passes):
+                nc.tensor.matmul_mx(out=acc[:], lhsT=lhs[0][:, mcol].bitcast(E5), lhsT_scale=lhs[1][:, mcol],
+                                    rhs=rhs[0][:, ncol].bitcast(E4), rhs_scale=rhs[1][:, ncol],
+                                    start=(s == 0), stop=(s == len(passes) - 1))
+            if kind == "dxa":
+                k = 4 * q + m
+                if k % 2 == 0 and nh == 0:
+                    part_t[k // 2] = work.tile([P, 2, C], F32, tag=("raw", "grp")[k // 2 % 2], align_bytes=64, name="part")
+                copy(out=part_t[k // 2][:, k % 2, ncol], in_=acc[:])
+                return
+            if nh == 0:
+                ostage[kind, q, m] = work.tile([P, C], F32, tag="out", bufs=4, name="out_m")
+            o = ostage[kind, q, m]
+            if kind == "dxb":
+                k = 4 * q + m
+                nc.vector.tensor_tensor(out=o[:, ncol], in0=acc[:], in1=part_t[k // 2][:, k % 2, ncol], op=ALU.add)
+                dst = o0_v[q, m]
+            else:
+                copy(out=o[:, ncol], in_=acc[:])
+                dst = o2_v[0, m] if q == 4 else o1_v[q, m]
+            if nh == 1:
+                nc.sync.dma_start(out=dst, in_=o[:])
+
+        wb, tb_raw = {}, {}
+        load_unit(0)
+        for nm, ap in (("q", qn_w), ("k", kn_w)):
+            t = const.tile([P, HD], BF16, name="w_" + nm)
+            nc.sync.dma_start(out=t[:], in_=ap.partition_broadcast(P))
+            wb[nm] = t
+        for nm, ap in (("cos", cos), ("sin", sin)):
+            t = const.tile([P, J, 64], BF16, name=nm + "_raw")
+            for half in range(2):
+                nc.sync.dma_start(out=t[64 * half : 64 * (half + 1), :, :], in_=ap.rearrange("(p j) i -> p j i", j=J))
+            tb_raw[nm] = t
+        load_saved(0)
+        ident_b = const.tile([P, P], BF16, name="ident_b")
+        make_identity(nc, ident_b[:])
+        ident_f = const.tile([P, P], F32, name="ident_f")
+        make_identity(nc, ident_f[:])
+        eps_t = const.tile([P, 1], F32, name="eps_t")
+        nc.vector.memset(eps_t[:], EPS)
+        warm = const.tile([P, 1], F32, name="warm")
+        nc.scalar.activation(out=warm[:], in_=eps_t[:], func=ACT.Sqrt)
+        load_unit(1)
+        load_saved(1)
+        load_item(0)
+
+        def make_diag(nm):
+            d = const.tile([P, HD], BF16, name="diag_" + nm)
+            nc.vector.tensor_tensor(out=d[:].rearrange("p (b x) -> p b x", b=2),
+                                    in0=ident_b[:].rearrange("p (x b) -> p b x", b=2),
+                                    in1=wb[nm][:].rearrange("p (x b) -> p b x", b=2), op=ALU.mult)
+            return d
+
+        diag_q = make_diag("q")
+        diag_k = make_diag("k")
+        tabb = const.tile([P, J, 2, 2, 2, 32], BF16, name="tabb")
+        for half in range(2):
+            for cs, nm, sign in ((0, "cos", -1.0), (1, "sin", -1.0 if half else 1.0)):
+                nc.vector.tensor_scalar(out=tabb[:, :, cs, :, half, :], in0=tb_raw[nm][:].rearrange("p j (i b) -> p j b i", b=2),
+                                        scalar1=sign, scalar2=None, op0=ALU.mult)
+        g_transposes(0, 0)
+        g_transposes(0, 1)
+        tabs = []
+        for k in range(2):
+            tt = psum.tile([P, 512], F32, tag="tab", name="tab%d" % k)
+            nc.tensor.matmul(tt[:], ident_b[:], tabb[:].rearrange("p j c b f i -> p (j c b f i)")[:, 512 * k : 512 * (k + 1)],
+                             start=True, stop=True)
+            tabs.append(tt)
+
+        total = J * UNITS
+        jobs = []
+        for q in range(4):
+            jobs += [(8 * q + 12, ("dw", q, m, nh)) for m in range(4) for nh in range(2)]
+        jobs += [(32 - 4 * g, ("dxa", g, m, nh)) for g in range(GROUPS) for m in range(4) for nh in range(2)]
+        jobs.sort(key=lambda job: job[0])
+        state = {"piece": 0, "job": 0}
+        ready = []
+
+        def slot(i):
+            n, j = divmod(i, J)
+            live = 0 <= i < total
+            if j == 0 and 2 <= n + 2 < UNITS:
+                load_unit(n + 2)
+                load_saved(n + 2)
+            if j == 2 and 0 <= n + 1 < UNITS:
+                inverse(n + 1)
+            if 0 <= i + 1 < total:
+                dots(i + 1)
+            if i + 6 < total:
+                ssq(i + 6)
+            if j == 1 and 0 <= n + 1 < UNITS:
+                root_mean_sq(n + 1)
+            if 0 <= i + 1 < total:
+                sums(i + 1)
+            if live:
+                project(i)
+                rope_products(i)
+            if j < 2 and n >= 0 and n + 1 < UNITS:
+                g_transposes(n + 1, j)
+            if j == 2 and n >= 1:
+                dz_transposes(n - 1)
+                dz_evacuate(n - 1, 0, nc.scalar.copy)
+                dz_evacuate(n - 1, 1, nc.scalar.copy)
+            if j == 3 and 1 <= n < UNITS - 1:
+                quant_tokens(n - 1)
+                quant_features(n - 1)
+            for rep in range(per_slot(i)):
+                if state["job"] < len(jobs) and jobs[state["job"]][0] <= i:
+                    mx_group(jobs[state["job"]][1], "mx", nc.scalar.copy)
+                    state["job"] += 1
+            if 0 <= i + 2 < total:
+                scaled_grad(i + 2)
+            if j == 3 and live and n < UNITS - 1:
+                for ib in range(2):
+                    for par in range(2):
+                        add_halves(n, par, ib, nc.gpsimd)
+            if live:
+                while state["piece"] < 28 and state["piece"] < 1.0 * (i + 1):
+                    interleave(state["piece"], piece_engine(state["piece"]))
+                    state["piece"] += 1
+                    if state["piece"] % 4 == 0:
+                        ready.append((i + ITEM_LAG, state["piece"] // 4 - 1))
+                if ready and ready[0][0] <= i:
+                    k = ready.pop(0)[1]
+                    quant_item(k)
+                    if k + 2 < 7:
+                        load_item(k + 2)
+
+        load_item(1)
+        for i in range(-6, total):
+            slot(i)
+
+        last = UNITS - 1
+        tags = ["mx", "a", "tab"]
+        count = [0]
+
+        def run(jobs_now):
+            for job in jobs_now:
+                mx_group(job, tags[(count[0] // 2) % 3], nc.scalar.copy)
+                count[0] += 1
+
+        for ib in range(2):
+            for par in range(2):
+                add_halves(last, par, ib, nc.vector)
+        quant_features(last - 1)
+        quant_tokens(last - 1)
+        run([job for when, job in jobs[state["job"] :] if job[0] == "dxa"])
+        dz_transposes(last)
+        dz_evacuate(last, 0, nc.scalar.copy)
+        dz_evacuate(last, 1, nc.scalar.copy)
+        run([("dxb", 0, m, nh) for m in range(2) for nh in range(2)])
+        quant_features(last)
+        quant_tokens(last)
+        run([job for when, job in jobs[state["job"] :] if job[0] == "dw"])
+        run([("dxb", 0, m, nh) for m in range(2, 4) for nh in range(2)])
+        for m in range(4):
+            run([("dxb", 1, m, nh) for nh in range(2)])
+            run([("dw", 4, m, nh) for nh in range(2)])

@@ -12,7 +12,13 @@ NH = 4
 GROUPS, QUADS = 2, 5
 UNITS = GROUPS * QUADS
 SPLIT = (4, 3)
-ITEM_LAG = 3
+ITEM_LAG = 4
+LOAD_LAG = 2
+GRP = 2
+ADD_PIECES = 2
+SUMS = 40
+DZ_SLOT, QT_SLOT, QF_SLOT = 3, 3, 1
+PIECE_RATE = 0.9
 W = 512
 FLOPS = 2 * 2 * TOKENS * (FQ + FK) * C
 BYTES = TOKENS * C * 2 + (FQ + FK) * C * 2 + TOKENS * (FQ + FK) * 6 + (TOKENS + FQ + FK) * C * 4
@@ -51,15 +57,16 @@ def tile_gqaselfattention_pa_v_kernel(tc, x, wq, bq, wk, bk, qn_w, kn_w, cos, si
         tokq, featq, trp = {}, {}, {}
         itemq, raw_t, grp_t = {}, {}, {}
         ostage, part_t = {}, {}
+        waiting = []
 
         def scalar_sums(i):
-            return i < 28
+            return i < SUMS
 
         def per_slot(i):
             return 1 if i < 27 else 2 + i % 2
 
         def piece_engine(piece):
-            return "S" if piece % 2 == 0 and piece < 8 else "G"
+            return "S" if piece % 2 == 0 else "G"
 
         def load_unit(n):
             q, g = divmod(n, GROUPS)
@@ -73,8 +80,8 @@ def tile_gqaselfattention_pa_v_kernel(tc, x, wq, bq, wk, bk, qn_w, kn_w, cos, si
             rr = work.tile([P, J, W], F32, tag="r", bufs=3)
             src_r = rk_v[g] if q == 4 else rq_v[g, :, :, W * q : W * (q + 1)]
             if n == 0:
-                for j in range(J):
-                    nc.sync.dma_start(out=rr[:, j, :], in_=src_r[:, j, :])
+                for j in range(0, J, 2):
+                    nc.sync.dma_start(out=rr[:, j : j + 2, :], in_=src_r[:, j : j + 2, :])
             else:
                 nc.sync.dma_start(out=rr[:], in_=src_r)
             r_t[n] = rr
@@ -123,7 +130,7 @@ def tile_gqaselfattention_pa_v_kernel(tc, x, wq, bq, wk, bk, qn_w, kn_w, cos, si
         def scaled_grad(i):
             n, j = divmod(i, J)
             a = psum.tile([P, NH, HD], F32, tag="a")
-            diag = diag_k if n // GROUPS == 4 else diag_q
+            diag = diags["k" if n // GROUPS == 4 else "q"]
             for h in range(NH):
                 nc.tensor.matmul(a[:, h, :], gt_t[n][:, NH * j + h, :], diag[:], start=True, stop=True)
             a_t[i] = a
@@ -183,8 +190,13 @@ def tile_gqaselfattention_pa_v_kernel(tc, x, wq, bq, wk, bk, qn_w, kn_w, cos, si
         def add_halves(n, par, ib, eng):
             if par == 0 and ib == 0:
                 dzt_t[n] = work.tile([P, 4, P, J], BF16, tag="dzt", align_bytes=64, name="dzt_n")
-            mv = m_t[n][:].rearrange("p j (c b f) h i -> p c b f (h i) j", c=2, b=2)
-            eng.tensor_tensor(out=dzt_t[n][:, 2 * ib + par], in0=mv[:, 0, ib, par], in1=mv[:, 1, ib, 1 - par], op=ALU.add)
+            mv = m_t[n][:].rearrange("p j q h i -> p j q (h i)").rearrange("p j q (y x) -> p q y j x", x=4)
+            k = 2 * ib + par
+            nsp = ADD_PIECES if eng is nc.gpsimd else 1
+            for y in range(nsp):
+                ys = slice(32 // nsp * y, 32 // nsp * (y + 1))
+                eng.tensor_tensor(out=dzt_t[n][:, k].rearrange("p (y x) j -> p y j x", x=4)[:, ys],
+                                  in0=mv[:, 2 * ib + par, ys], in1=mv[:, 4 + 2 * ib + 1 - par, ys], op=ALU.add)
 
         def quant_tokens(n):
             codes = work.tile([P, 4 * P], U32, tag="tokc", bufs=4, align_bytes=64)
@@ -213,7 +225,7 @@ def tile_gqaselfattention_pa_v_kernel(tc, x, wq, bq, wk, bk, qn_w, kn_w, cos, si
             featq[n] = (codes, scales)
 
         def load_item(k):
-            raw = work.tile([P, J, C], BF16, tag="raw", align_bytes=64)
+            raw = work.tile([P, J, C], BF16, tag="raw", bufs=2, align_bytes=64)
             src = x_v[k] if k < 2 else (wk_v[0] if k == 6 else wq_v[k - 2])
             nc.sync.dma_start(out=raw[:], in_=src)
             raw_t[k] = raw
@@ -221,14 +233,15 @@ def tile_gqaselfattention_pa_v_kernel(tc, x, wq, bq, wk, bk, qn_w, kn_w, cos, si
         def interleave(piece, eng):
             k, s = divmod(piece, 4)
             if s == 0:
-                grp_t[k] = work.tile([P, C, J], BF16, tag="grp", align_bytes=64, name="grp_k")
+                grp_t[k] = work.tile([P, C, J], BF16, tag="grp", bufs=GRP, align_bytes=64, name="grp_k")
             c0 = 256 * s
             if eng == "S":
                 nc.scalar.copy(out=grp_t[k][:, c0 : c0 + 256, :].rearrange("p (c i) t -> p c t i", i=4),
                                in_=raw_t[k][:, :, c0 : c0 + 256].rearrange("p t (c i) -> p c t i", i=4))
             else:
-                nc.gpsimd.tensor_scalar(out=grp_t[k][:, c0 : c0 + 256, :], in0=raw_t[k][:, :, c0 : c0 + 256].rearrange("p t c -> p c t"),
-                                        scalar1=1.0, scalar2=0.0, op0=ALU.mult, op1=ALU.add)
+                for c1 in range(c0, c0 + 256, 128):
+                    nc.gpsimd.tensor_scalar(out=grp_t[k][:, c1 : c1 + 128, :], in0=raw_t[k][:, :, c1 : c1 + 128].rearrange("p t c -> p c t"),
+                                            scalar1=1.0, scalar2=0.0, op0=ALU.mult, op1=ALU.add)
 
         def quant_item(k):
             codes = const.tile([P, C], U32, align_bytes=64, name="itemc%d" % k)
@@ -237,6 +250,7 @@ def tile_gqaselfattention_pa_v_kernel(tc, x, wq, bq, wk, bk, qn_w, kn_w, cos, si
             itemq[k] = (codes, scales)
 
         def mx_group(job, tag, copy):
+            flush_stores()
             kind, q, m, nh = job
             acc = psum.tile([P, 512], F32, tag=tag, name="acc")
             ncol = slice(512 * nh, 512 * (nh + 1))
@@ -253,7 +267,7 @@ def tile_gqaselfattention_pa_v_kernel(tc, x, wq, bq, wk, bk, qn_w, kn_w, cos, si
             if kind == "dxa":
                 k = 4 * q + m
                 if k % 2 == 0 and nh == 0:
-                    part_t[k // 2] = work.tile([P, 2, C], F32, tag=("raw", "grp")[k // 2 % 2], align_bytes=64, name="part")
+                    part_t[k // 2] = work.tile([P, 2, C], F32, tag=("raw", "grp")[k // 2 % 2], bufs=(2, GRP)[k // 2 % 2], align_bytes=64, name="part")
                 copy(out=part_t[k // 2][:, k % 2, ncol], in_=acc[:])
                 return
             if nh == 0:
@@ -267,20 +281,31 @@ def tile_gqaselfattention_pa_v_kernel(tc, x, wq, bq, wk, bk, qn_w, kn_w, cos, si
                 copy(out=o[:, ncol], in_=acc[:])
                 dst = o2_v[0, m] if q == 4 else o1_v[q, m]
             if nh == 1:
-                nc.sync.dma_start(out=dst, in_=o[:])
+                if kind == "dxb":
+                    nc.sync.dma_start(out=dst, in_=o[:])
+                else:
+                    waiting.append((dst, o))
+
+        def flush_stores():
+            while waiting:
+                dst, o = waiting.pop(0)
+                nc.scalar.dma_start(out=dst, in_=o[:])
 
         wb, tb_raw = {}, {}
-        load_unit(0)
-        for nm, ap in (("q", qn_w), ("k", kn_w)):
+
+        def load_gain(nm, ap):
             t = const.tile([P, HD], BF16, name="w_" + nm)
             nc.sync.dma_start(out=t[:], in_=ap.partition_broadcast(P))
             wb[nm] = t
+
+        load_unit(0)
+        load_gain("q", qn_w)
+        load_saved(0)
         for nm, ap in (("cos", cos), ("sin", sin)):
             t = const.tile([P, J, 64], BF16, name=nm + "_raw")
             for half in range(2):
                 nc.sync.dma_start(out=t[64 * half : 64 * (half + 1), :, :], in_=ap.rearrange("(p j) i -> p j i", j=J))
             tb_raw[nm] = t
-        load_saved(0)
         ident_b = const.tile([P, P], BF16, name="ident_b")
         make_identity(nc, ident_b[:])
         ident_f = const.tile([P, P], F32, name="ident_f")
@@ -291,6 +316,7 @@ def tile_gqaselfattention_pa_v_kernel(tc, x, wq, bq, wk, bk, qn_w, kn_w, cos, si
         nc.scalar.activation(out=warm[:], in_=eps_t[:], func=ACT.Sqrt)
         load_unit(1)
         load_saved(1)
+        load_gain("k", kn_w)
         load_item(0)
 
         def make_diag(nm):
@@ -300,8 +326,7 @@ def tile_gqaselfattention_pa_v_kernel(tc, x, wq, bq, wk, bk, qn_w, kn_w, cos, si
                                     in1=wb[nm][:].rearrange("p (x b) -> p b x", b=2), op=ALU.mult)
             return d
 
-        diag_q = make_diag("q")
-        diag_k = make_diag("k")
+        diags = {"q": make_diag("q")}
         tabb = const.tile([P, J, 2, 2, 2, 32], BF16, name="tabb")
         for half in range(2):
             for cs, nm, sign in ((0, "cos", -1.0), (1, "sin", -1.0 if half else 1.0)):
@@ -322,8 +347,15 @@ def tile_gqaselfattention_pa_v_kernel(tc, x, wq, bq, wk, bk, qn_w, kn_w, cos, si
             jobs += [(8 * q + 12, ("dw", q, m, nh)) for m in range(4) for nh in range(2)]
         jobs += [(32 - 4 * g, ("dxa", g, m, nh)) for g in range(GROUPS) for m in range(4) for nh in range(2)]
         jobs.sort(key=lambda job: job[0])
-        state = {"piece": 0, "job": 0}
-        ready = []
+        state = {"job": 0}
+        item_quants, item_loads, piece_slots = {}, {}, {}
+        for pc in range(28):
+            at = int(pc / PIECE_RATE)
+            piece_slots.setdefault(at, []).append(pc)
+            if pc % 4 == 3:
+                item_quants.setdefault(at + ITEM_LAG, []).append(pc // 4)
+                if pc // 4 + 2 < 7:
+                    item_loads.setdefault(at + LOAD_LAG, []).append(pc // 4 + 2)
 
         def slot(i):
             n, j = divmod(i, J)
@@ -335,24 +367,27 @@ def tile_gqaselfattention_pa_v_kernel(tc, x, wq, bq, wk, bk, qn_w, kn_w, cos, si
                 inverse(n + 1)
             if 0 <= i + 1 < total:
                 dots(i + 1)
+            if i < 2 and 0 <= i + 1 < total:
+                sums(i + 1)
             if i + 6 < total:
                 ssq(i + 6)
             if j == 1 and 0 <= n + 1 < UNITS:
                 root_mean_sq(n + 1)
-            if 0 <= i + 1 < total:
+            if 2 <= i and i + 1 < total:
                 sums(i + 1)
             if live:
                 project(i)
                 rope_products(i)
             if j < 2 and n >= 0 and n + 1 < UNITS:
                 g_transposes(n + 1, j)
-            if j == 2 and n >= 1:
+            if j == DZ_SLOT and n >= 1:
                 dz_transposes(n - 1)
                 dz_evacuate(n - 1, 0, nc.scalar.copy)
                 dz_evacuate(n - 1, 1, nc.scalar.copy)
-            if j == 3 and 1 <= n < UNITS - 1:
+            if j == QT_SLOT and 1 <= n < UNITS - 1:
                 quant_tokens(n - 1)
-                quant_features(n - 1)
+            if j == QF_SLOT and 2 <= n < UNITS:
+                quant_features(n - 2)
             for rep in range(per_slot(i)):
                 if state["job"] < len(jobs) and jobs[state["job"]][0] <= i:
                     mx_group(jobs[state["job"]][1], "mx", nc.scalar.copy)
@@ -363,21 +398,18 @@ def tile_gqaselfattention_pa_v_kernel(tc, x, wq, bq, wk, bk, qn_w, kn_w, cos, si
                 for ib in range(2):
                     for par in range(2):
                         add_halves(n, par, ib, nc.gpsimd)
-            if live:
-                while state["piece"] < 28 and state["piece"] < 1.0 * (i + 1):
-                    interleave(state["piece"], piece_engine(state["piece"]))
-                    state["piece"] += 1
-                    if state["piece"] % 4 == 0:
-                        ready.append((i + ITEM_LAG, state["piece"] // 4 - 1))
-                if ready and ready[0][0] <= i:
-                    k = ready.pop(0)[1]
-                    quant_item(k)
-                    if k + 2 < 7:
-                        load_item(k + 2)
+            for k in item_quants.get(i, ()):
+                quant_item(k)
+            for k in item_loads.get(i, ()):
+                load_item(k)
+            for pc in piece_slots.get(i, ()):
+                interleave(pc, piece_engine(pc))
 
         load_item(1)
         for i in range(-6, total):
             slot(i)
+            if i == 0:
+                diags["k"] = make_diag("k")
 
         last = UNITS - 1
         tags = ["mx", "a", "tab"]
@@ -393,15 +425,15 @@ def tile_gqaselfattention_pa_v_kernel(tc, x, wq, bq, wk, bk, qn_w, kn_w, cos, si
                 add_halves(last, par, ib, nc.vector)
         quant_features(last - 1)
         quant_tokens(last - 1)
-        run([job for when, job in jobs[state["job"] :] if job[0] == "dxa"])
+        run([job for when, job in jobs[state["job"] :]])
         dz_transposes(last)
         dz_evacuate(last, 0, nc.scalar.copy)
         dz_evacuate(last, 1, nc.scalar.copy)
         run([("dxb", 0, m, nh) for m in range(2) for nh in range(2)])
         quant_features(last)
         quant_tokens(last)
-        run([job for when, job in jobs[state["job"] :] if job[0] == "dw"])
         run([("dxb", 0, m, nh) for m in range(2, 4) for nh in range(2)])
         for m in range(4):
             run([("dxb", 1, m, nh) for nh in range(2)])
             run([("dw", 4, m, nh) for nh in range(2)])
+        flush_stores()

@@ -3,37 +3,46 @@ from contextlib import ExitStack
 import concourse.mybir as mybir
 from concourse.masks import make_identity
 
-P = 128
-TOKENS, C, HD = 1024, 1024, 128
-FQ, FK = 2048, 512
+TOKENS, C = 1024, 1024
+HD, FQ, FK = 128, 2048, 512
 EPS = 1e-6
+P = 128
 J = 4
 NH = 4
+W = NH * HD
 GROUPS, QUADS = 2, 5
 UNITS = GROUPS * QUADS
-SPLIT = (4, 3)
-ITEM_LAG = 4
-LOAD_LAG = 2
-GRP = 2
-ADD_PIECES = 2
-SUMS = 40
-DZ_SLOT, QT_SLOT, QF_SLOT = 3, 3, 1
-PIECE_RATE = 0.9
-W = 512
+STEPS = J * UNITS
+
 FLOPS = 2 * 2 * TOKENS * (FQ + FK) * C
 BYTES = TOKENS * C * 2 + (FQ + FK) * C * 2 + TOKENS * (FQ + FK) * 6 + (TOKENS + FQ + FK) * C * 4
+
+EARLY = 3
+EARLY_FROM = (32, 26)
+
+A_BANKS, T_BANKS = 3, 3
 
 F32 = mybir.dt.float32
 BF16 = mybir.dt.bfloat16
 U32 = mybir.dt.uint32
 U8 = mybir.dt.uint8
-E4 = mybir.dt.float8_e4m3fn_x4
-E5 = mybir.dt.float8_e5m2_x4
+E4M3 = mybir.dt.float8_e4m3fn_x4
+E5M2 = mybir.dt.float8_e5m2_x4
 ALU = mybir.AluOpType
 ACT = mybir.ActivationFunctionType
 
 
-def tile_gqaselfattention_pa_v_kernel(tc, x, wq, bq, wk, bk, qn_w, kn_w, cos, sin, rq, rk, grad_0, grad_1, out_0, out_1, out_2):
+def sums_on_scalar(i):
+    return i < 26 and i % 2 == 0
+
+
+def products_in_step(i):
+    return 1 if i < 26 else 2 if i < 32 else 3 if i < 38 else 1
+
+
+def tile_gqaselfattention_pa_v_kernel(
+    tc, x, wq, bq, wk, bk, qn_w, kn_w, cos, sin, rq, rk, grad_0, grad_1, out_0, out_1, out_2
+):
     nc = tc.nc
     rq_v = rq.rearrange("b t h d -> (b t) (h d)").rearrange("(g p j) f -> g p j f", p=P, j=J)
     rk_v = rk.rearrange("b t h d -> (b t) (h d)").rearrange("(g p j) f -> g p j f", p=P, j=J)
@@ -52,388 +61,340 @@ def tile_gqaselfattention_pa_v_kernel(tc, x, wq, bq, wk, bk, qn_w, kn_w, cos, si
         psum = ctx.enter_context(tc.psum_pool(name="psum", bufs=2))
         ctx.enter_context(tc.manual_schedule())
 
-        r_t, g_t, gt_t, a_t, ssq_t, std_t, inv_t, nq_t = {}, {}, {}, {}, {}, {}, {}, {}
-        dot_t, nk_t, d0_t, m_t, dzt_t, dzf_t = {}, {}, {}, {}, {}, {}
-        tokq, featq, trp = {}, {}, {}
-        itemq, raw_t, grp_t = {}, {}, {}
-        ostage, part_t = {}, {}
-        waiting = []
+        grad_t, saved_t, turned_t, ssq_t, std_t, inv_t, inv2_t = {}, {}, {}, {}, {}, {}, {}
+        scaled_t, prod_t, coef_t, proj_t, roped_t, summed_t = {}, {}, {}, {}, {}, {}
+        feat_t, tok_t, feat_q, tok_q = {}, {}, {}, {}
+        raw_t, grouped_t, operand_q = {}, {}, {}
+        early_t, out_t, gain_t, diag_t, table_t = {}, {}, {}, {}, {}
+        to_store = []
 
-        def scalar_sums(i):
-            return i < SUMS
-
-        def per_slot(i):
-            return 1 if i < 27 else 2 + i % 2
-
-        def piece_engine(piece):
-            return "S" if piece % 2 == 0 else "G"
-
-        def load_unit(n):
+        def load_grad(n):
             q, g = divmod(n, GROUPS)
-            gg = work.tile([P, J, W], BF16, tag="g", bufs=3)
-            src_g = gk_v[g] if q == 4 else gq_v[g, :, :, W * q : W * (q + 1)]
-            nc.sync.dma_start(out=gg[:], in_=src_g)
-            g_t[n] = gg
+            t = work.tile([P, J, W], BF16, tag="grad", bufs=3)
+            nc.sync.dma_start(out=t[:], in_=gk_v[g] if q == 4 else gq_v[g, :, :, W * q : W * (q + 1)])
+            grad_t[n] = t
 
         def load_saved(n):
             q, g = divmod(n, GROUPS)
-            rr = work.tile([P, J, W], F32, tag="r", bufs=3)
-            src_r = rk_v[g] if q == 4 else rq_v[g, :, :, W * q : W * (q + 1)]
-            if n == 0:
-                for j in range(0, J, 2):
-                    nc.sync.dma_start(out=rr[:, j : j + 2, :], in_=src_r[:, j : j + 2, :])
-            else:
-                nc.sync.dma_start(out=rr[:], in_=src_r)
-            r_t[n] = rr
+            t = work.tile([P, J, W], F32, tag="saved", bufs=3)
+            src = rk_v[g] if q == 4 else rq_v[g, :, :, W * q : W * (q + 1)]
+            cuts = 2 if n == 0 else 1
+            for c in range(cuts):
+                js = slice(J // cuts * c, J // cuts * (c + 1))
+                nc.sync.dma_start(out=t[:, js, :], in_=src[:, js, :])
+            saved_t[n] = t
 
-        def r_perm(n, j, h):
-            return r_t[n][:, j, HD * h : HD * (h + 1)].rearrange("p (x b) -> p b x", b=2)
+        def load_gain(kind, src):
+            t = const.tile([P, HD], BF16, name="gain_" + kind)
+            nc.sync.dma_start(out=t[:], in_=src.partition_broadcast(P))
+            gain_t[kind] = t
 
-        def ssq(i):
+        def load_operand(k):
+            t = work.tile([P, J, C], BF16, tag="raw", align_bytes=64)
+            nc.sync.dma_start(out=t[:], in_=x_v[k] if k < 2 else wk_v[0] if k == 6 else wq_v[k - 2])
+            raw_t[k] = t
+
+        def squares(i):
             n, j = divmod(i, J)
             if j == 0:
-                ssq_t[n] = work.tile([P, J * NH], F32, tag="ssq", name="ssq_n")
+                ssq_t[n] = work.tile([P, J * NH], F32, tag="ssq", name="ssq")
             for h in range(NH):
-                k = NH * j + h
+                r = saved_t[n][:, j, HD * h : HD * (h + 1)]
+                total = ssq_t[n][:, NH * j + h : NH * j + h + 1]
                 if n == 0 and j % 2 == 1:
-                    junk = work.tile([P, HD], F32, tag="junk_v", bufs=2)
-                    rv = r_t[n][:, j, HD * h : HD * (h + 1)]
-                    nc.vector.scalar_tensor_tensor(out=junk[:], in0=rv, scalar=1.0, in1=rv, op0=ALU.mult, op1=ALU.mult,
-                                                   accum_out=ssq_t[n][:, k : k + 1])
-                    continue
-                junk = work.tile([P, HD], BF16, tag="junk_s", bufs=2)
-                nc.scalar.activation(out=junk[:], in_=r_t[n][:, j, HD * h : HD * (h + 1)], func=ACT.Square,
-                                     accum_out=ssq_t[n][:, k : k + 1])
+                    unused = work.tile([P, HD], F32, tag="unused_v", bufs=4)
+                    nc.vector.scalar_tensor_tensor(out=unused[:], in0=r, scalar=1.0, in1=r, op0=ALU.mult, op1=ALU.mult, accum_out=total)
+                else:
+                    unused = work.tile([P, HD], BF16, tag="unused_s", bufs=8)
+                    nc.scalar.activation(out=unused[:], in_=r, func=ACT.Square, accum_out=total)
 
-        def root_mean_sq(n):
-            std = work.tile([P, J * NH], F32, tag="std")
-            nc.scalar.activation(out=std[:], in_=ssq_t[n][:], func=ACT.Sqrt, scale=1.0 / HD, bias=eps_t[:])
-            std_t[n] = std
+        def root(n):
+            t = work.tile([P, J * NH], F32, tag="std")
+            nc.scalar.activation(out=t[:], in_=ssq_t[n][:], func=ACT.Sqrt, scale=1.0 / HD, bias=eps[:])
+            std_t[n] = t
 
         def inverse(n):
-            inv = work.tile([P, J * NH], F32, tag="inv")
-            nc.vector.reciprocal(out=inv[:], in_=std_t[n][:])
-            inv_t[n] = inv
-            nq = work.tile([P, J * NH], F32, tag="nq")
-            nc.scalar.activation(out=nq[:], in_=inv[:], func=ACT.Square, scale=HD ** -0.5)
-            nq_t[n] = nq
+            inv_t[n] = work.tile([P, J * NH], F32, tag="inv", name="inv")
+            nc.vector.reciprocal(out=inv_t[n][:], in_=std_t[n][:])
+            inv2_t[n] = work.tile([P, J * NH], F32, tag="inv2", name="inv2")
+            nc.scalar.activation(out=inv2_t[n][:], in_=inv_t[n][:], func=ACT.Square, scale=HD**-0.5)
 
-        def g_transposes(n, half):
+        def turn_grad(n, half):
             if half == 0:
-                gt_t[n] = work.tile([P, J * NH, P], BF16, tag="gt", name="gt_n")
-            tp = psum.tile([P, 8, P], BF16, tag="tr")
+                turned_t[n] = work.tile([P, J * NH, P], BF16, tag="turned", name="turned")
+            bank = psum.tile([P, 8, P], BF16, tag="t", bufs=T_BANKS)
             for k in range(8):
                 j, h = divmod(8 * half + k, NH)
-                nc.tensor.transpose(tp[:, k, :], g_t[n][:, j, HD * h : HD * (h + 1)], ident_b[:])
-            nc.scalar.copy(out=gt_t[n][:, 8 * half : 8 * (half + 1), :], in_=tp[:])
+                nc.tensor.transpose(bank[:, k, :], grad_t[n][:, j, HD * h : HD * (h + 1)], ident_b[:])
+            nc.scalar.copy(out=turned_t[n][:, 8 * half : 8 * (half + 1), :], in_=bank[:])
 
-        def scaled_grad(i):
+        def make_diag(kind):
+            t = const.tile([P, HD], BF16, name="diag_" + kind)
+            nc.vector.tensor_tensor(
+                out=t[:].rearrange("p (b x) -> p b x", b=2), in0=ident_b[:].rearrange("p (x b) -> p b x", b=2),
+                in1=gain_t[kind][:].rearrange("p (x b) -> p b x", b=2), op=ALU.mult)
+            diag_t[kind] = t
+
+        def scale_grad(i):
             n, j = divmod(i, J)
-            a = psum.tile([P, NH, HD], F32, tag="a")
-            diag = diags["k" if n // GROUPS == 4 else "q"]
+            bank = psum.tile([P, NH, HD], F32, tag="a", bufs=A_BANKS)
+            diag = diag_t["k" if n // GROUPS == 4 else "q"]
             for h in range(NH):
-                nc.tensor.matmul(a[:, h, :], gt_t[n][:, NH * j + h, :], diag[:], start=True, stop=True)
-            a_t[i] = a
+                nc.tensor.matmul(bank[:, h, :], turned_t[n][:, NH * j + h, :], diag[:], start=True, stop=True)
+            scaled_t[i] = bank
 
-        def a_perm(i, h):
-            return a_t[i][:, h, :].rearrange("p (b x) -> p b x", b=2)
+        def a_of(i, h):
+            return scaled_t[i][:, h, :].rearrange("p (b x) -> p b x", b=2)
 
-        def dots(i):
+        def r_of(i, h):
             n, j = divmod(i, J)
-            nk = work.tile([P, NH], F32, tag="nk", bufs=3)
-            nk_t[i] = nk
-            if scalar_sums(i):
-                pr = work.tile([P, NH, HD], F32, tag="prod")
-                nc.vector.tensor_tensor(out=pr[:].rearrange("p h (b x) -> p h b x", b=2),
-                                        in0=a_t[i][:].rearrange("p h (b x) -> p h b x", b=2),
-                                        in1=r_t[n][:, j, :].rearrange("p (h x b) -> p h b x", h=NH, b=2), op=ALU.mult)
-                dot_t[i] = pr
+            return saved_t[n][:, j, HD * h : HD * (h + 1)].rearrange("p (x b) -> p b x", b=2)
+
+        def dot_products(i):
+            n, j = divmod(i, J)
+            coef_t[i] = work.tile([P, NH], F32, tag="coef", bufs=3, name="coef")
+            if sums_on_scalar(i):
+                prod_t[i] = work.tile([P, NH, HD], F32, tag="prod", name="prod")
+                nc.vector.tensor_tensor(
+                    out=prod_t[i][:].rearrange("p h (b x) -> p h b x", b=2), in0=scaled_t[i][:].rearrange("p h (b x) -> p h b x", b=2),
+                    in1=saved_t[n][:, j, :].rearrange("p (h x b) -> p h b x", h=NH, b=2), op=ALU.mult)
                 return
             for h in range(NH):
                 k = NH * j + h
-                junk = work.tile([P, HD], F32, tag="junk_v", bufs=2)
+                unused = work.tile([P, HD], F32, tag="unused_v", bufs=4)
                 nc.vector.scalar_tensor_tensor(
-                    out=junk[:].rearrange("p (b x) -> p b x", b=2), in0=a_perm(i, h), scalar=nq_t[n][:, k : k + 1],
-                    in1=r_perm(n, j, h), op0=ALU.mult, op1=ALU.mult, accum_out=nk[:, h : h + 1])
+                    out=unused[:].rearrange("p (b x) -> p b x", b=2), in0=a_of(i, h), scalar=inv2_t[n][:, k : k + 1], in1=r_of(i, h),
+                    op0=ALU.mult, op1=ALU.mult, accum_out=coef_t[i][:, h : h + 1])
 
-        def sums(i):
-            if not scalar_sums(i):
-                return
+        def sum_products(i):
             n, j = divmod(i, J)
             for h in range(NH):
                 k = NH * j + h
-                junk = work.tile([P, HD], BF16, tag="junk_s", bufs=2)
-                nc.scalar.activation(out=junk[:], in_=dot_t[i][:, h, :], func=ACT.Copy, scale=nq_t[n][:, k : k + 1],
-                                     accum_out=nk_t[i][:, h : h + 1])
+                unused = work.tile([P, HD], BF16, tag="unused_s", bufs=8)
+                nc.scalar.activation(
+                    out=unused[:], in_=prod_t[i][:, h, :], func=ACT.Copy, scale=inv2_t[n][:, k : k + 1], accum_out=coef_t[i][:, h : h + 1])
 
         def project(i):
-            n, j = divmod(i, J)
-            d0 = work.tile([P, NH, HD], F32, tag="d0")
+            proj_t[i] = work.tile([P, NH, HD], F32, tag="proj", name="proj")
             for h in range(NH):
                 nc.vector.scalar_tensor_tensor(
-                    out=d0[:, h, :].rearrange("p (b x) -> p b x", b=2), in0=r_perm(n, j, h), scalar=nk_t[i][:, h : h + 1],
-                    in1=a_perm(i, h), op0=ALU.mult, op1=ALU.subtract)
-            d0_t[i] = d0
+                    out=proj_t[i][:, h, :].rearrange("p (b x) -> p b x", b=2), in0=r_of(i, h), scalar=coef_t[i][:, h : h + 1], in1=a_of(i, h),
+                    op0=ALU.mult, op1=ALU.subtract)
 
         def rope_products(i):
             n, j = divmod(i, J)
-            if j == 0:
-                m_t[n] = work.tile([P, J, 8, NH, 32], F32, tag="m", name="m_n")
+            roped_t[i] = work.tile([P, 8, NH, 32], F32, tag="roped", bufs=3, name="roped")
+            table = table_t[j // 2][:, 256 * (j % 2) : 256 * (j % 2 + 1)].rearrange("p (s k y) -> p s k y", s=2, y=32)
             for h in range(NH):
-                k = NH * j + h
-                d = d0_t[i][:, h : h + 1, :].to_broadcast([P, 2, HD]).rearrange("p c (q i) -> p c q i", i=32)
-                tb = tabs[j // 2][:, 256 * (j % 2) : 256 * (j % 2 + 1)].rearrange("p (c q i) -> p c q i", c=2, i=32)
                 nc.vector.scalar_tensor_tensor(
-                    out=m_t[n][:, j, :, h, :].rearrange("p (c q) i -> p c q i", c=2), in0=d, scalar=inv_t[n][:, k : k + 1],
-                    in1=tb, op0=ALU.mult, op1=ALU.mult)
+                    out=roped_t[i][:, :, h, :].rearrange("p (s k) y -> p s k y", s=2),
+                    in0=proj_t[i][:, h : h + 1, :].to_broadcast([P, 2, HD]).rearrange("p s (k y) -> p s k y", y=32),
+                    scalar=inv_t[n][:, NH * j + h : NH * j + h + 1], in1=table, op0=ALU.mult, op1=ALU.mult)
 
-        def add_halves(n, par, ib, eng):
-            if par == 0 and ib == 0:
-                dzt_t[n] = work.tile([P, 4, P, J], BF16, tag="dzt", align_bytes=64, name="dzt_n")
-            mv = m_t[n][:].rearrange("p j q h i -> p j q (h i)").rearrange("p j q (y x) -> p q y j x", x=4)
-            k = 2 * ib + par
-            nsp = ADD_PIECES if eng is nc.gpsimd else 1
-            for y in range(nsp):
-                ys = slice(32 // nsp * y, 32 // nsp * (y + 1))
-                eng.tensor_tensor(out=dzt_t[n][:, k].rearrange("p (y x) j -> p y j x", x=4)[:, ys],
-                                  in0=mv[:, 2 * ib + par, ys], in1=mv[:, 4 + 2 * ib + 1 - par, ys], op=ALU.add)
+        def rope_sums(i):
+            bank = psum.tile([P, 4, P], F32, tag="t", bufs=T_BANKS)
+            for t in range(4):
+                b, odd = divmod(t, 2)
+                for last, k in enumerate((2 * b + odd, 4 + 2 * b + 1 - odd)):
+                    nc.tensor.matmul(
+                        bank[:, t, :], roped_t[i][:, k].rearrange("p h y -> p (h y)"), ident_f[:],
+                        start=(last == 0), stop=(last == 1), is_transpose=True)
+            summed_t[i] = bank
 
-        def quant_tokens(n):
-            codes = work.tile([P, 4 * P], U32, tag="tokc", bufs=4, align_bytes=64)
-            scales = work.tile([P, 4 * P], U8, tag="toks", bufs=4, align_bytes=64)
-            nc.vector.quantize_mx(out=codes[:].bitcast(E5), scales=scales[:], in_=dzt_t[n][:].rearrange("p t x j -> p (t x j)"))
-            tokq[n] = (codes, scales)
+        def round_features(i):
+            n, j = divmod(i, J)
+            if j == 0:
+                feat_t[n] = work.tile([P, J * P, 4], BF16, tag="feat", align_bytes=64, name="feat")
+            nc.scalar.copy(out=feat_t[n][:, P * j : P * (j + 1), :], in_=summed_t[i][:].rearrange("p t x -> p x t"))
 
-        def dz_transposes(n):
-            words = dzt_t[n][:].rearrange("p t x j -> p (t x j)").bitcast(F32).rearrange("p (t x u) -> p t x u", t=4, u=2)
+        def turn_back(n):
+            words = feat_t[n][:].rearrange("p x t -> p (x t)").bitcast(F32).rearrange("p (x u) -> p x u", u=2)
+            tok_t[n] = work.tile([P, 4, P, J], BF16, tag="tok", align_bytes=64, name="tok")
             for u in range(2):
-                tp = psum.tile([P, 4, P], F32, tag="tr")
-                for t in range(4):
-                    nc.tensor.transpose(tp[:, t, :], words[:, t, :, u], ident_f[:])
-                trp[n, u] = tp
+                bank = psum.tile([P, J, P], F32, tag="t", bufs=T_BANKS)
+                for j in range(J):
+                    nc.tensor.transpose(bank[:, j, :], words[:, P * j : P * (j + 1), u], ident_f[:])
+                nc.scalar.copy(
+                    out=tok_t[n][:, 2 * u : 2 * u + 2],
+                    in_=bank[:].rearrange("p j m -> p (j m)").bitcast(BF16).rearrange("p (j m e) -> p e m j", j=J, e=2))
 
-        def dz_evacuate(n, u, copy):
-            if u == 0:
-                dzf_t[n] = work.tile([P, 4 * P, 4], BF16, tag="dzf", align_bytes=64, name="dzf_n")
-            pv = trp[n, u][:].rearrange("p t x -> p (t x)").bitcast(BF16).rearrange("p (t x e) -> p e x t", t=4, e=2)
-            copy(out=dzf_t[n][:, 2 * P * u : 2 * P * (u + 1), :].rearrange("p (e x) t -> p e x t", e=2), in_=pv)
+        def quantise_features(n):
+            codes = const.tile([P, J * P], U32, align_bytes=64, name="feat_codes_%d" % n)
+            scales = const.tile([P, J * P], U8, align_bytes=64, name="feat_scales_%d" % n)
+            nc.vector.quantize_mx(out=codes[:].bitcast(E5M2), scales=scales[:], in_=feat_t[n][:].rearrange("p x t -> p (x t)"))
+            feat_q[n] = (codes, scales)
 
-        def quant_features(n):
-            codes = const.tile([P, 4 * P], U32, align_bytes=64, name="featc%d" % n)
-            scales = const.tile([P, 4 * P], U8, align_bytes=64, name="feats%d" % n)
-            nc.vector.quantize_mx(out=codes[:].bitcast(E5), scales=scales[:], in_=dzf_t[n][:].rearrange("p x t -> p (x t)"))
-            featq[n] = (codes, scales)
+        def quantise_tokens(n):
+            codes = work.tile([P, 4 * P], U32, tag="tok_codes", bufs=4, align_bytes=64)
+            scales = work.tile([P, 4 * P], U8, tag="tok_scales", bufs=4, align_bytes=64)
+            nc.vector.quantize_mx(out=codes[:].bitcast(E5M2), scales=scales[:], in_=tok_t[n][:].rearrange("p t m j -> p (t m j)"))
+            tok_q[n] = (codes, scales)
 
-        def load_item(k):
-            raw = work.tile([P, J, C], BF16, tag="raw", bufs=2, align_bytes=64)
-            src = x_v[k] if k < 2 else (wk_v[0] if k == 6 else wq_v[k - 2])
-            nc.sync.dma_start(out=raw[:], in_=src)
-            raw_t[k] = raw
+        def interleave(k, quarter):
+            if quarter == 0:
+                grouped_t[k] = work.tile([P, C, J], BF16, tag="grouped", align_bytes=64, name="grouped")
+            for c in range(256 * quarter, 256 * (quarter + 1), 128):
+                nc.gpsimd.tensor_scalar(
+                    out=grouped_t[k][:, c : c + 128, :], in0=raw_t[k][:, :, c : c + 128].rearrange("p j c -> p c j"),
+                    scalar1=1.0, scalar2=0.0, op0=ALU.mult, op1=ALU.add)
 
-        def interleave(piece, eng):
-            k, s = divmod(piece, 4)
-            if s == 0:
-                grp_t[k] = work.tile([P, C, J], BF16, tag="grp", bufs=GRP, align_bytes=64, name="grp_k")
-            c0 = 256 * s
-            if eng == "S":
-                nc.scalar.copy(out=grp_t[k][:, c0 : c0 + 256, :].rearrange("p (c i) t -> p c t i", i=4),
-                               in_=raw_t[k][:, :, c0 : c0 + 256].rearrange("p t (c i) -> p c t i", i=4))
-            else:
-                for c1 in range(c0, c0 + 256, 128):
-                    nc.gpsimd.tensor_scalar(out=grp_t[k][:, c1 : c1 + 128, :], in0=raw_t[k][:, :, c1 : c1 + 128].rearrange("p t c -> p c t"),
-                                            scalar1=1.0, scalar2=0.0, op0=ALU.mult, op1=ALU.add)
-
-        def quant_item(k):
-            codes = const.tile([P, C], U32, align_bytes=64, name="itemc%d" % k)
-            scales = const.tile([P, C], U8, align_bytes=64, name="items%d" % k)
-            nc.vector.quantize_mx(out=codes[:].bitcast(E4), scales=scales[:], in_=grp_t[k][:].rearrange("p c t -> p (c t)"))
-            itemq[k] = (codes, scales)
-
-        def mx_group(job, tag, copy):
-            flush_stores()
-            kind, q, m, nh = job
-            acc = psum.tile([P, 512], F32, tag=tag, name="acc")
-            ncol = slice(512 * nh, 512 * (nh + 1))
-            mcol = slice(P * m, P * (m + 1))
-            if kind == "dw":
-                passes = [(tokq[GROUPS * q + g], itemq[g]) for g in range(GROUPS)]
-            else:
-                ks = range(SPLIT[q]) if kind == "dxa" else range(SPLIT[q], QUADS)
-                passes = [(featq[GROUPS * k + q], itemq[2 + k]) for k in ks]
-            for s, (lhs, rhs) in enumerate(passes):
-                nc.tensor.matmul_mx(out=acc[:], lhsT=lhs[0][:, mcol].bitcast(E5), lhsT_scale=lhs[1][:, mcol],
-                                    rhs=rhs[0][:, ncol].bitcast(E4), rhs_scale=rhs[1][:, ncol],
-                                    start=(s == 0), stop=(s == len(passes) - 1))
-            if kind == "dxa":
-                k = 4 * q + m
-                if k % 2 == 0 and nh == 0:
-                    part_t[k // 2] = work.tile([P, 2, C], F32, tag=("raw", "grp")[k // 2 % 2], bufs=(2, GRP)[k // 2 % 2], align_bytes=64, name="part")
-                copy(out=part_t[k // 2][:, k % 2, ncol], in_=acc[:])
-                return
-            if nh == 0:
-                ostage[kind, q, m] = work.tile([P, C], F32, tag="out", bufs=4, name="out_m")
-            o = ostage[kind, q, m]
-            if kind == "dxb":
-                k = 4 * q + m
-                nc.vector.tensor_tensor(out=o[:, ncol], in0=acc[:], in1=part_t[k // 2][:, k % 2, ncol], op=ALU.add)
-                dst = o0_v[q, m]
-            else:
-                copy(out=o[:, ncol], in_=acc[:])
-                dst = o2_v[0, m] if q == 4 else o1_v[q, m]
-            if nh == 1:
-                if kind == "dxb":
-                    nc.sync.dma_start(out=dst, in_=o[:])
-                else:
-                    waiting.append((dst, o))
+        def quantise_operand(k):
+            codes = const.tile([P, C], U32, align_bytes=64, name="operand_codes_%d" % k)
+            scales = const.tile([P, C], U8, align_bytes=64, name="operand_scales_%d" % k)
+            nc.vector.quantize_mx(out=codes[:].bitcast(E4M3), scales=scales[:], in_=grouped_t[k][:].rearrange("p c j -> p (c j)"))
+            operand_q[k] = (codes, scales)
 
         def flush_stores():
-            while waiting:
-                dst, o = waiting.pop(0)
-                nc.scalar.dma_start(out=dst, in_=o[:])
+            while to_store:
+                dst, t = to_store.pop(0)
+                nc.scalar.dma_start(out=dst, in_=t[:])
 
-        wb, tb_raw = {}, {}
+        def product(job, tag, banks):
+            flush_stores()
+            kind, s, m, half = job
+            cols = slice(512 * half, 512 * (half + 1))
+            rows = slice(P * m, P * (m + 1))
+            if kind == "dw":
+                passes = [(tok_q[GROUPS * s + g], operand_q[g]) for g in range(GROUPS)]
+            else:
+                quads = range(EARLY) if kind == "early" else range(EARLY, QUADS)
+                passes = [(feat_q[GROUPS * q + s], operand_q[2 + q]) for q in quads]
+            bank = psum.tile([P, 512], F32, tag=tag, bufs=banks)
+            for k, (left, right) in enumerate(passes):
+                nc.tensor.matmul_mx(
+                    out=bank[:], lhsT=left[0][:, rows].bitcast(E5M2), lhsT_scale=left[1][:, rows], rhs=right[0][:, cols].bitcast(E4M3),
+                    rhs_scale=right[1][:, cols], start=(k == 0), stop=(k == len(passes) - 1))
+            if kind == "early":
+                pair, place = divmod(4 * s + m, 2)
+                if place == 0 and half == 0:
+                    early_t[pair] = work.tile([P, 2, C], F32, tag=("raw", "early")[s], align_bytes=64, name="early")
+                nc.scalar.copy(out=early_t[pair][:, place, cols], in_=bank[:])
+                return
+            if half == 0:
+                out_t[job[:3]] = work.tile([P, C], F32, tag="out", bufs=3, name="out")
+            t = out_t[job[:3]]
+            if kind == "late":
+                pair, place = divmod(4 * s + m, 2)
+                nc.vector.tensor_tensor(out=t[:, cols], in0=bank[:], in1=early_t[pair][:, place, cols], op=ALU.add)
+                if half == 1:
+                    nc.sync.dma_start(out=o0_v[s, m], in_=t[:])
+            else:
+                nc.scalar.copy(out=t[:, cols], in_=bank[:])
+                if half == 1:
+                    to_store.append((o2_v[0, m] if s == 4 else o1_v[s, m], t))
 
-        def load_gain(nm, ap):
-            t = const.tile([P, HD], BF16, name="w_" + nm)
-            nc.sync.dma_start(out=t[:], in_=ap.partition_broadcast(P))
-            wb[nm] = t
-
-        load_unit(0)
+        load_grad(0)
         load_gain("q", qn_w)
+        trig = {}
+        for name, src in (("cos", cos), ("sin", sin)):
+            trig[name] = const.tile([P, J, 64], BF16, name=name)
+            nc.vector.memset(trig[name][:], 0.0)
+            nc.sync.dma_start(out=trig[name][0:64, :, :], in_=src.rearrange("(p j) y -> p j y", j=J))
         load_saved(0)
-        for nm, ap in (("cos", cos), ("sin", sin)):
-            t = const.tile([P, J, 64], BF16, name=nm + "_raw")
-            for half in range(2):
-                nc.sync.dma_start(out=t[64 * half : 64 * (half + 1), :, :], in_=ap.rearrange("(p j) i -> p j i", j=J))
-            tb_raw[nm] = t
         ident_b = const.tile([P, P], BF16, name="ident_b")
         make_identity(nc, ident_b[:])
         ident_f = const.tile([P, P], F32, name="ident_f")
         make_identity(nc, ident_f[:])
-        eps_t = const.tile([P, 1], F32, name="eps_t")
-        nc.vector.memset(eps_t[:], EPS)
-        warm = const.tile([P, 1], F32, name="warm")
-        nc.scalar.activation(out=warm[:], in_=eps_t[:], func=ACT.Sqrt)
-        load_unit(1)
+        eps = const.tile([P, 1], F32, name="eps")
+        nc.vector.memset(eps[:], EPS)
+        loaded = const.tile([P, 1], F32, name="loaded")
+        nc.scalar.activation(out=loaded[:], in_=eps[:], func=ACT.Sqrt)
+        load_grad(1)
         load_saved(1)
         load_gain("k", kn_w)
-        load_item(0)
+        load_operand(0)
+        make_diag("q")
 
-        def make_diag(nm):
-            d = const.tile([P, HD], BF16, name="diag_" + nm)
-            nc.vector.tensor_tensor(out=d[:].rearrange("p (b x) -> p b x", b=2),
-                                    in0=ident_b[:].rearrange("p (x b) -> p b x", b=2),
-                                    in1=wb[nm][:].rearrange("p (x b) -> p b x", b=2), op=ALU.mult)
-            return d
-
-        diags = {"q": make_diag("q")}
-        tabb = const.tile([P, J, 2, 2, 2, 32], BF16, name="tabb")
-        for half in range(2):
-            for cs, nm, sign in ((0, "cos", -1.0), (1, "sin", -1.0 if half else 1.0)):
-                nc.vector.tensor_scalar(out=tabb[:, :, cs, :, half, :], in0=tb_raw[nm][:].rearrange("p j (i b) -> p j b i", b=2),
-                                        scalar1=sign, scalar2=None, op0=ALU.mult)
-        g_transposes(0, 0)
-        g_transposes(0, 1)
-        tabs = []
+        twice = const.tile([P, P], BF16, name="twice")
+        for f in range(2):
+            nc.vector.tensor_copy(out=twice[:, 64 * f : 64 * (f + 1)], in_=ident_b[:, 0:64])
+        signed = const.tile([P, J, 2, 2, 2, 32], BF16, name="signed")
+        for f in range(2):
+            for s, name, sign in ((0, "cos", -1.0), (1, "sin", 1.0 - 2.0 * f)):
+                nc.vector.tensor_scalar(
+                    out=signed[:, :, s, :, f, :], in0=trig[name][:].rearrange("p j (y b) -> p j b y", b=2), scalar1=sign, scalar2=None, op0=ALU.mult)
+        turn_grad(0, 0)
+        turn_grad(0, 1)
         for k in range(2):
-            tt = psum.tile([P, 512], F32, tag="tab", name="tab%d" % k)
-            nc.tensor.matmul(tt[:], ident_b[:], tabb[:].rearrange("p j c b f i -> p (j c b f i)")[:, 512 * k : 512 * (k + 1)],
-                             start=True, stop=True)
-            tabs.append(tt)
+            table_t[k] = psum.tile([P, 512], F32, tag="table", name="table")
+            nc.tensor.matmul(
+                table_t[k][:], twice[:], signed[:].rearrange("p j s b f y -> p (j s b f y)")[:, 512 * k : 512 * (k + 1)], start=True, stop=True)
+        load_operand(1)
 
-        total = J * UNITS
-        jobs = []
-        for q in range(4):
-            jobs += [(8 * q + 12, ("dw", q, m, nh)) for m in range(4) for nh in range(2)]
-        jobs += [(32 - 4 * g, ("dxa", g, m, nh)) for g in range(GROUPS) for m in range(4) for nh in range(2)]
+        jobs = [(max(12, 8 * q + 11), ("dw", q, t, half)) for q in range(4) for t in range(4) for half in range(2)]
+        jobs += [(EARLY_FROM[g], ("early", g, j, half)) for g in range(GROUPS) for j in range(J) for half in range(2)]
         jobs.sort(key=lambda job: job[0])
-        state = {"job": 0}
-        item_quants, item_loads, piece_slots = {}, {}, {}
-        for pc in range(28):
-            at = int(pc / PIECE_RATE)
-            piece_slots.setdefault(at, []).append(pc)
-            if pc % 4 == 3:
-                item_quants.setdefault(at + ITEM_LAG, []).append(pc // 4)
-                if pc // 4 + 2 < 7:
-                    item_loads.setdefault(at + LOAD_LAG, []).append(pc // 4 + 2)
+        squares_at = {}
+        for i in range(STEPS):
+            squares_at.setdefault(-6 if i < 4 else max(i - 6, (i - 4) // 2), []).append(i)
+        quantise_at = {4 * k + 7: k for k in range(7)}
+        load_at = {4 * k + 5: k + 2 for k in range(5)}
 
-        def slot(i):
+        for i in range(-6, STEPS):
             n, j = divmod(i, J)
-            live = 0 <= i < total
             if j == 0 and 2 <= n + 2 < UNITS:
-                load_unit(n + 2)
+                load_grad(n + 2)
                 load_saved(n + 2)
-            if j == 2 and 0 <= n + 1 < UNITS:
-                inverse(n + 1)
-            if 0 <= i + 1 < total:
-                dots(i + 1)
-            if i < 2 and 0 <= i + 1 < total:
-                sums(i + 1)
-            if i + 6 < total:
-                ssq(i + 6)
+            if 0 <= i + 1 < STEPS:
+                dot_products(i + 1)
+            if i >= 2:
+                rope_sums(i - 2)
+            if i < 2 and i + 1 >= 0 and sums_on_scalar(i + 1):
+                sum_products(i + 1)
+            for k in squares_at.get(i, ()):
+                squares(k)
             if j == 1 and 0 <= n + 1 < UNITS:
-                root_mean_sq(n + 1)
-            if 2 <= i and i + 1 < total:
-                sums(i + 1)
-            if live:
+                root(n + 1)
+            if i >= 2 and i + 1 < STEPS and sums_on_scalar(i + 1):
+                sum_products(i + 1)
+            if i >= 2:
+                round_features(i - 2)
+            if i >= 0:
                 project(i)
                 rope_products(i)
-            if j < 2 and n >= 0 and n + 1 < UNITS:
-                g_transposes(n + 1, j)
-            if j == DZ_SLOT and n >= 1:
-                dz_transposes(n - 1)
-                dz_evacuate(n - 1, 0, nc.scalar.copy)
-                dz_evacuate(n - 1, 1, nc.scalar.copy)
-            if j == QT_SLOT and 1 <= n < UNITS - 1:
-                quant_tokens(n - 1)
-            if j == QF_SLOT and 2 <= n < UNITS:
-                quant_features(n - 2)
-            for rep in range(per_slot(i)):
-                if state["job"] < len(jobs) and jobs[state["job"]][0] <= i:
-                    mx_group(jobs[state["job"]][1], "mx", nc.scalar.copy)
-                    state["job"] += 1
-            if 0 <= i + 2 < total:
-                scaled_grad(i + 2)
-            if j == 3 and live and n < UNITS - 1:
-                for ib in range(2):
-                    for par in range(2):
-                        add_halves(n, par, ib, nc.gpsimd)
-            for k in item_quants.get(i, ()):
-                quant_item(k)
-            for k in item_loads.get(i, ()):
-                load_item(k)
-            for pc in piece_slots.get(i, ()):
-                interleave(pc, piece_engine(pc))
-
-        load_item(1)
-        for i in range(-6, total):
-            slot(i)
+            if j == 2 and 0 <= n + 1 < UNITS:
+                inverse(n + 1)
+            if j < 2 and 0 <= n and n + 1 < UNITS:
+                turn_grad(n + 1, j)
+            if j == 2 and n >= 1:
+                turn_back(n - 1)
+            for k in range(products_in_step(i)):
+                if jobs and jobs[0][0] <= i:
+                    product(jobs.pop(0)[1], "t", T_BANKS)
+            if 0 <= i + A_BANKS < STEPS:
+                scale_grad(i + A_BANKS)
+            if j == 2 and n >= 1:
+                quantise_features(n - 1)
+            if j == 3 and n >= 1:
+                quantise_tokens(n - 1)
+            if i in quantise_at:
+                quantise_operand(quantise_at[i])
+            if i in load_at:
+                load_operand(load_at[i])
+            if 0 <= i < 28:
+                interleave(i // 4, i % 4)
             if i == 0:
-                diags["k"] = make_diag("k")
+                make_diag("k")
 
-        last = UNITS - 1
-        tags = ["mx", "a", "tab"]
-        count = [0]
+        for i in range(STEPS - 2, STEPS):
+            rope_sums(i)
+            round_features(i)
+        banks = [("t", T_BANKS), ("t", T_BANKS), ("a", A_BANKS), ("table", 2)]
+        turn = [0]
 
-        def run(jobs_now):
-            for job in jobs_now:
-                mx_group(job, tags[(count[0] // 2) % 3], nc.scalar.copy)
-                count[0] += 1
+        def products(now):
+            for job in now:
+                tag, count = banks[turn[0] // 2 % 4]
+                product(job, tag, count)
+                turn[0] += 1
 
-        for ib in range(2):
-            for par in range(2):
-                add_halves(last, par, ib, nc.vector)
-        quant_features(last - 1)
-        quant_tokens(last - 1)
-        run([job for when, job in jobs[state["job"] :]])
-        dz_transposes(last)
-        dz_evacuate(last, 0, nc.scalar.copy)
-        dz_evacuate(last, 1, nc.scalar.copy)
-        run([("dxb", 0, m, nh) for m in range(2) for nh in range(2)])
-        quant_features(last)
-        quant_tokens(last)
-        run([("dxb", 0, m, nh) for m in range(2, 4) for nh in range(2)])
+        products([job for first, job in jobs])
+        products([("late", 0, j, half) for j in range(2) for half in range(2)])
+        quantise_features(UNITS - 1)
+        turn_back(UNITS - 1)
+        products([("late", 0, j, half) for j in range(2, 4) for half in range(2)])
+        quantise_tokens(UNITS - 1)
         for m in range(4):
-            run([("dxb", 1, m, nh) for nh in range(2)])
-            run([("dw", 4, m, nh) for nh in range(2)])
+            products([("late", 1, m, half) for half in range(2)])
+            products([("dw", 4, m, half) for half in range(2)])
         flush_stores()

from contextlib import ExitStack

import concourse.mybir as mybir
from concourse.masks import make_identity

TOKENS, C = 1024, 1024
HD, FQ, FK = 128, 2048, 512
EPS = 1e-6
P = 128
J = 4
NH = 4
W = NH * HD
GROUPS, QUADS = 2, 5
UNITS = GROUPS * QUADS
STEPS = J * UNITS

FLOPS = 2 * 2 * TOKENS * (FQ + FK) * C
BYTES = TOKENS * C * 2 + (FQ + FK) * C * 2 + TOKENS * (FQ + FK) * 6 + (TOKENS + FQ + FK) * C * 4

EARLY = 3
EARLY_FROM = (32, 26)

A_BANKS, T_BANKS = 3, 3

F32 = mybir.dt.float32
BF16 = mybir.dt.bfloat16
U32 = mybir.dt.uint32
U8 = mybir.dt.uint8
E4M3 = mybir.dt.float8_e4m3fn_x4
E5M2 = mybir.dt.float8_e5m2_x4
ALU = mybir.AluOpType
ACT = mybir.ActivationFunctionType


def sums_on_scalar(i):
    return i < 26 and i % 2 == 0


def products_in_step(i):
    return 1 if i < 26 else 2 if i < 32 else 3 if i < 38 else 1


def tile_gqaselfattention_pa_v_kernel(
    tc, x, wq, bq, wk, bk, qn_w, kn_w, cos, sin, rq, rk, grad_0, grad_1, out_0, out_1, out_2
):
    nc = tc.nc
    rq_v = rq.rearrange("b t h d -> (b t) (h d)").rearrange("(g p j) f -> g p j f", p=P, j=J)
    rk_v = rk.rearrange("b t h d -> (b t) (h d)").rearrange("(g p j) f -> g p j f", p=P, j=J)
    gq_v = grad_0.rearrange("b t h d -> (b t) (h d)").rearrange("(g p j) f -> g p j f", p=P, j=J)
    gk_v = grad_1.rearrange("b t h d -> (b t) (h d)").rearrange("(g p j) f -> g p j f", p=P, j=J)
    x_v = x.rearrange("b t c -> (b t) c").rearrange("(g p j) c -> g p j c", p=P, j=J)
    wq_v = wq.rearrange("(q p j) c -> q p j c", p=P, j=J)
    wk_v = wk.rearrange("(q p j) c -> q p j c", p=P, j=J)
    o0_v = out_0.rearrange("b t c -> (b t) c").rearrange("(g m j) c -> g j m c", m=P, j=J)
    o1_v = out_1.rearrange("(q m t) c -> q t m c", m=P, t=4)
    o2_v = out_2.rearrange("(q m t) c -> q t m c", m=P, t=4)

    with ExitStack() as ctx:
        const = ctx.enter_context(tc.tile_pool(name="const", bufs=1))
        work = ctx.enter_context(tc.tile_pool(name="work", bufs=2))
        psum = ctx.enter_context(tc.psum_pool(name="psum", bufs=2))
        ctx.enter_context(tc.manual_schedule())

        grad_t, saved_t, turned_t, ssq_t, std_t, inv_t, inv2_t = {}, {}, {}, {}, {}, {}, {}
        scaled_t, prod_t, coef_t, proj_t, roped_t, summed_t = {}, {}, {}, {}, {}, {}
        feat_t, tok_t, feat_q, tok_q = {}, {}, {}, {}
        raw_t, grouped_t, operand_q = {}, {}, {}
        early_t, out_t, gain_t, diag_t, table_t = {}, {}, {}, {}, {}
        to_store = []

        def load_grad(n):
            q, g = divmod(n, GROUPS)
            t = work.tile([P, J, W], BF16, tag="grad", bufs=3)
            nc.sync.dma_start(out=t[:], in_=gk_v[g] if q == 4 else gq_v[g, :, :, W * q : W * (q + 1)])
            grad_t[n] = t

        def load_saved(n):
            q, g = divmod(n, GROUPS)
            t = work.tile([P, J, W], F32, tag="saved", bufs=3)
            src = rk_v[g] if q == 4 else rq_v[g, :, :, W * q : W * (q + 1)]
            cuts = 2 if n == 0 else 1
            for c in range(cuts):
                js = slice(J // cuts * c, J // cuts * (c + 1))
                nc.sync.dma_start(out=t[:, js, :], in_=src[:, js, :])
            saved_t[n] = t

        def load_gain(kind, src):
            t = const.tile([P, HD], BF16, name="gain_" + kind)
            nc.sync.dma_start(out=t[:], in_=src.partition_broadcast(P))
            gain_t[kind] = t

        def load_operand(k):
            t = work.tile([P, J, C], BF16, tag="raw", align_bytes=64)
            nc.sync.dma_start(out=t[:], in_=x_v[k] if k < 2 else wk_v[0] if k == 6 else wq_v[k - 2])
            raw_t[k] = t

        def squares(i):
            n, j = divmod(i, J)
            if j == 0:
                ssq_t[n] = work.tile([P, J * NH], F32, tag="ssq", name="ssq")
            for h in range(NH):
                r = saved_t[n][:, j, HD * h : HD * (h + 1)]
                total = ssq_t[n][:, NH * j + h : NH * j + h + 1]
                if n == 0 and j % 2 == 1:
                    unused = work.tile([P, HD], F32, tag="unused_v", bufs=4)
                    nc.vector.scalar_tensor_tensor(out=unused[:], in0=r, scalar=1.0, in1=r, op0=ALU.mult, op1=ALU.mult, accum_out=total)
                else:
                    unused = work.tile([P, HD], BF16, tag="unused_s", bufs=8)
                    nc.scalar.activation(out=unused[:], in_=r, func=ACT.Square, accum_out=total)

        def root(n):
            t = work.tile([P, J * NH], F32, tag="std")
            nc.scalar.activation(out=t[:], in_=ssq_t[n][:], func=ACT.Sqrt, scale=1.0 / HD, bias=eps[:])
            std_t[n] = t

        def inverse(n):
            inv_t[n] = work.tile([P, J * NH], F32, tag="inv", name="inv")
            nc.vector.reciprocal(out=inv_t[n][:], in_=std_t[n][:])
            inv2_t[n] = work.tile([P, J * NH], F32, tag="inv2", name="inv2")
            nc.scalar.activation(out=inv2_t[n][:], in_=inv_t[n][:], func=ACT.Square, scale=HD**-0.5)

        def turn_grad(n, half):
            if half == 0:
                turned_t[n] = work.tile([P, J * NH, P], BF16, tag="turned", name="turned")
            bank = psum.tile([P, 8, P], BF16, tag="t", bufs=T_BANKS)
            for k in range(8):
                j, h = divmod(8 * half + k, NH)
                nc.tensor.transpose(bank[:, k, :], grad_t[n][:, j, HD * h : HD * (h + 1)], ident_b[:])
            nc.scalar.copy(out=turned_t[n][:, 8 * half : 8 * (half + 1), :], in_=bank[:])

        def make_diag(kind):
            t = const.tile([P, HD], BF16, name="diag_" + kind)
            nc.vector.tensor_tensor(
                out=t[:].rearrange("p (b x) -> p b x", b=2), in0=ident_b[:].rearrange("p (x b) -> p b x", b=2),
                in1=gain_t[kind][:].rearrange("p (x b) -> p b x", b=2), op=ALU.mult)
            diag_t[kind] = t

        def scale_grad(i):
            n, j = divmod(i, J)
            bank = psum.tile([P, NH, HD], F32, tag="a", bufs=A_BANKS)
            diag = diag_t["k" if n // GROUPS == 4 else "q"]
            for h in range(NH):
                nc.tensor.matmul(bank[:, h, :], turned_t[n][:, NH * j + h, :], diag[:], start=True, stop=True)
            scaled_t[i] = bank

        def a_of(i, h):
            return scaled_t[i][:, h, :].rearrange("p (b x) -> p b x", b=2)

        def r_of(i, h):
            n, j = divmod(i, J)
            return saved_t[n][:, j, HD * h : HD * (h + 1)].rearrange("p (x b) -> p b x", b=2)

        def dot_products(i):
            n, j = divmod(i, J)
            coef_t[i] = work.tile([P, NH], F32, tag="coef", bufs=3, name="coef")
            if sums_on_scalar(i):
                prod_t[i] = work.tile([P, NH, HD], F32, tag="prod", name="prod")
                nc.vector.tensor_tensor(
                    out=prod_t[i][:].rearrange("p h (b x) -> p h b x", b=2), in0=scaled_t[i][:].rearrange("p h (b x) -> p h b x", b=2),
                    in1=saved_t[n][:, j, :].rearrange("p (h x b) -> p h b x", h=NH, b=2), op=ALU.mult)
                return
            for h in range(NH):
                k = NH * j + h
                unused = work.tile([P, HD], F32, tag="unused_v", bufs=4)
                nc.vector.scalar_tensor_tensor(
                    out=unused[:].rearrange("p (b x) -> p b x", b=2), in0=a_of(i, h), scalar=inv2_t[n][:, k : k + 1], in1=r_of(i, h),
                    op0=ALU.mult, op1=ALU.mult, accum_out=coef_t[i][:, h : h + 1])

        def sum_products(i):
            n, j = divmod(i, J)
            for h in range(NH):
                k = NH * j + h
                unused = work.tile([P, HD], BF16, tag="unused_s", bufs=8)
                nc.scalar.activation(
                    out=unused[:], in_=prod_t[i][:, h, :], func=ACT.Copy, scale=inv2_t[n][:, k : k + 1], accum_out=coef_t[i][:, h : h + 1])

        def project(i):
            proj_t[i] = work.tile([P, NH, HD], F32, tag="proj", name="proj")
            for h in range(NH):
                nc.vector.scalar_tensor_tensor(
                    out=proj_t[i][:, h, :].rearrange("p (b x) -> p b x", b=2), in0=r_of(i, h), scalar=coef_t[i][:, h : h + 1], in1=a_of(i, h),
                    op0=ALU.mult, op1=ALU.subtract)

        def rope_products(i):
            n, j = divmod(i, J)
            roped_t[i] = work.tile([P, 8, NH, 32], F32, tag="roped", bufs=3, name="roped")
            table = table_t[j // 2][:, 256 * (j % 2) : 256 * (j % 2 + 1)].rearrange("p (s k y) -> p s k y", s=2, y=32)
            for h in range(NH):
                nc.vector.scalar_tensor_tensor(
                    out=roped_t[i][:, :, h, :].rearrange("p (s k) y -> p s k y", s=2),
                    in0=proj_t[i][:, h : h + 1, :].to_broadcast([P, 2, HD]).rearrange("p s (k y) -> p s k y", y=32),
                    scalar=inv_t[n][:, NH * j + h : NH * j + h + 1], in1=table, op0=ALU.mult, op1=ALU.mult)

        def rope_sums(i):
            bank = psum.tile([P, 4, P], F32, tag="t", bufs=T_BANKS)
            for t in range(4):
                b, odd = divmod(t, 2)
                for last, k in enumerate((2 * b + odd, 4 + 2 * b + 1 - odd)):
                    nc.tensor.matmul(
                        bank[:, t, :], roped_t[i][:, k].rearrange("p h y -> p (h y)"), ident_f[:],
                        start=(last == 0), stop=(last == 1), is_transpose=True)
            summed_t[i] = bank

        def round_features(i):
            n, j = divmod(i, J)
            if j == 0:
                feat_t[n] = work.tile([P, J * P, 4], BF16, tag="feat", align_bytes=64, name="feat")
            nc.scalar.copy(out=feat_t[n][:, P * j : P * (j + 1), :], in_=summed_t[i][:].rearrange("p t x -> p x t"))

        def turn_back(n):
            words = feat_t[n][:].rearrange("p x t -> p (x t)").bitcast(F32).rearrange("p (x u) -> p x u", u=2)
            tok_t[n] = work.tile([P, 4, P, J], BF16, tag="tok", align_bytes=64, name="tok")
            for u in range(2):
                bank = psum.tile([P, J, P], F32, tag="t", bufs=T_BANKS)
                for j in range(J):
                    nc.tensor.transpose(bank[:, j, :], words[:, P * j : P * (j + 1), u], ident_f[:])
                nc.scalar.copy(
                    out=tok_t[n][:, 2 * u : 2 * u + 2],
                    in_=bank[:].rearrange("p j m -> p (j m)").bitcast(BF16).rearrange("p (j m e) -> p e m j", j=J, e=2))

        def quantise_features(n):
            codes = const.tile([P, J * P], U32, align_bytes=64, name="feat_codes_%d" % n)
            scales = const.tile([P, J * P], U8, align_bytes=64, name="feat_scales_%d" % n)
            nc.vector.quantize_mx(out=codes[:].bitcast(E5M2), scales=scales[:], in_=feat_t[n][:].rearrange("p x t -> p (x t)"))
            feat_q[n] = (codes, scales)

        def quantise_tokens(n):
            codes = work.tile([P, 4 * P], U32, tag="tok_codes", bufs=4, align_bytes=64)
            scales = work.tile([P, 4 * P], U8, tag="tok_scales", bufs=4, align_bytes=64)
            nc.vector.quantize_mx(out=codes[:].bitcast(E5M2), scales=scales[:], in_=tok_t[n][:].rearrange("p t m j -> p (t m j)"))
            tok_q[n] = (codes, scales)

        def interleave(k, quarter):
            if quarter == 0:
                grouped_t[k] = work.tile([P, C, J], BF16, tag="grouped", align_bytes=64, name="grouped")
            for c in range(256 * quarter, 256 * (quarter + 1), 128):
                nc.gpsimd.tensor_scalar(
                    out=grouped_t[k][:, c : c + 128, :], in0=raw_t[k][:, :, c : c + 128].rearrange("p j c -> p c j"),
                    scalar1=1.0, scalar2=0.0, op0=ALU.mult, op1=ALU.add)

        def quantise_operand(k):
            codes = const.tile([P, C], U32, align_bytes=64, name="operand_codes_%d" % k)
            scales = const.tile([P, C], U8, align_bytes=64, name="operand_scales_%d" % k)
            nc.vector.quantize_mx(out=codes[:].bitcast(E4M3), scales=scales[:], in_=grouped_t[k][:].rearrange("p c j -> p (c j)"))
            operand_q[k] = (codes, scales)

        def flush_stores():
            while to_store:
                dst, t = to_store.pop(0)
                nc.scalar.dma_start(out=dst, in_=t[:])

        def product(job, tag, banks):
            flush_stores()
            kind, s, m, half = job
            cols = slice(512 * half, 512 * (half + 1))
            rows = slice(P * m, P * (m + 1))
            if kind == "dw":
                passes = [(tok_q[GROUPS * s + g], operand_q[g]) for g in range(GROUPS)]
            else:
                quads = range(EARLY) if kind == "early" else range(EARLY, QUADS)
                passes = [(feat_q[GROUPS * q + s], operand_q[2 + q]) for q in quads]
            bank = psum.tile([P, 512], F32, tag=tag, bufs=banks)
            for k, (left, right) in enumerate(passes):
                nc.tensor.matmul_mx(
                    out=bank[:], lhsT=left[0][:, rows].bitcast(E5M2), lhsT_scale=left[1][:, rows], rhs=right[0][:, cols].bitcast(E4M3),
                    rhs_scale=right[1][:, cols], start=(k == 0), stop=(k == len(passes) - 1))
            if kind == "early":
                pair, place = divmod(4 * s + m, 2)
                if place == 0 and half == 0:
                    early_t[pair] = work.tile([P, 2, C], F32, tag=("raw", "early")[s], align_bytes=64, name="early")
                nc.scalar.copy(out=early_t[pair][:, place, cols], in_=bank[:])
                return
            if half == 0:
                out_t[job[:3]] = work.tile([P, C], F32, tag="out", bufs=3, name="out")
            t = out_t[job[:3]]
            if kind == "late":
                pair, place = divmod(4 * s + m, 2)
                nc.vector.tensor_tensor(out=t[:, cols], in0=bank[:], in1=early_t[pair][:, place, cols], op=ALU.add)
                if half == 1:
                    nc.sync.dma_start(out=o0_v[s, m], in_=t[:])
            else:
                nc.scalar.copy(out=t[:, cols], in_=bank[:])
                if half == 1:
                    to_store.append((o2_v[0, m] if s == 4 else o1_v[s, m], t))

        load_grad(0)
        load_gain("q", qn_w)
        trig = {}
        for name, src in (("cos", cos), ("sin", sin)):
            trig[name] = const.tile([P, J, 64], BF16, name=name)
            nc.vector.memset(trig[name][:], 0.0)
            nc.sync.dma_start(out=trig[name][0:64, :, :], in_=src.rearrange("(p j) y -> p j y", j=J))
        load_saved(0)
        ident_b = const.tile([P, P], BF16, name="ident_b")
        make_identity(nc, ident_b[:])
        ident_f = const.tile([P, P], F32, name="ident_f")
        make_identity(nc, ident_f[:])
        eps = const.tile([P, 1], F32, name="eps")
        nc.vector.memset(eps[:], EPS)
        loaded = const.tile([P, 1], F32, name="loaded")
        nc.scalar.activation(out=loaded[:], in_=eps[:], func=ACT.Sqrt)
        load_grad(1)
        load_saved(1)
        load_gain("k", kn_w)
        load_operand(0)
        make_diag("q")

        twice = const.tile([P, P], BF16, name="twice")
        for f in range(2):
            nc.vector.tensor_copy(out=twice[:, 64 * f : 64 * (f + 1)], in_=ident_b[:, 0:64])
        signed = const.tile([P, J, 2, 2, 2, 32], BF16, name="signed")
        for f in range(2):
            for s, name, sign in ((0, "cos", -1.0), (1, "sin", 1.0 - 2.0 * f)):
                nc.vector.tensor_scalar(
                    out=signed[:, :, s, :, f, :], in0=trig[name][:].rearrange("p j (y b) -> p j b y", b=2), scalar1=sign, scalar2=None, op0=ALU.mult)
        turn_grad(0, 0)
        turn_grad(0, 1)
        for k in range(2):
            table_t[k] = psum.tile([P, 512], F32, tag="table", name="table")
            nc.tensor.matmul(
                table_t[k][:], twice[:], signed[:].rearrange("p j s b f y -> p (j s b f y)")[:, 512 * k : 512 * (k + 1)], start=True, stop=True)
        load_operand(1)

        jobs = [(max(12, 8 * q + 11), ("dw", q, t, half)) for q in range(4) for t in range(4) for half in range(2)]
        jobs += [(EARLY_FROM[g], ("early", g, j, half)) for g in range(GROUPS) for j in range(J) for half in range(2)]
        jobs.sort(key=lambda job: job[0])
        squares_at = {}
        for i in range(STEPS):
            squares_at.setdefault(-6 if i < 4 else max(i - 6, (i - 4) // 2), []).append(i)
        quantise_at = {4 * k + 7: k for k in range(7)}
        load_at = {4 * k + 5: k + 2 for k in range(5)}

        for i in range(-6, STEPS):
            n, j = divmod(i, J)
            if j == 0 and 2 <= n + 2 < UNITS:
                load_grad(n + 2)
                load_saved(n + 2)
            if 0 <= i + 1 < STEPS:
                dot_products(i + 1)
            if i >= 2:
                rope_sums(i - 2)
            if i < 2 and i + 1 >= 0 and sums_on_scalar(i + 1):
                sum_products(i + 1)
            for k in squares_at.get(i, ()):
                squares(k)
            if j == 1 and 0 <= n + 1 < UNITS:
                root(n + 1)
            if i >= 2 and i + 1 < STEPS and sums_on_scalar(i + 1):
                sum_products(i + 1)
            if i >= 2:
                round_features(i - 2)
            if i >= 0:
                project(i)
                rope_products(i)
            if j == 2 and 0 <= n + 1 < UNITS:
                inverse(n + 1)
            if j < 2 and 0 <= n and n + 1 < UNITS:
                turn_grad(n + 1, j)
            if j == 2 and n >= 1:
                turn_back(n - 1)
            for k in range(products_in_step(i)):
                if jobs and jobs[0][0] <= i:
                    product(jobs.pop(0)[1], "t", T_BANKS)
            if 0 <= i + A_BANKS < STEPS:
                scale_grad(i + A_BANKS)
            if j == 2 and n >= 1:
                quantise_features(n - 1)
            if j == 3 and n >= 1:
                quantise_tokens(n - 1)
            if i in quantise_at:
                quantise_operand(quantise_at[i])
            if i in load_at:
                load_operand(load_at[i])
            if 0 <= i < 28:
                interleave(i // 4, i % 4)
            if i == 0:
                make_diag("k")

        for i in range(STEPS - 2, STEPS):
            rope_sums(i)
            round_features(i)
        banks = [("t", T_BANKS), ("t", T_BANKS), ("a", A_BANKS), ("table", 2)]
        turn = [0]

        def products(now):
            for job in now:
                tag, count = banks[turn[0] // 2 % 4]
                product(job, tag, count)
                turn[0] += 1

        products([job for first, job in jobs])
        products([("late", 0, j, half) for j in range(2) for half in range(2)])
        quantise_features(UNITS - 1)
        turn_back(UNITS - 1)
        products([("late", 0, j, half) for j in range(2, 4) for half in range(2)])
        quantise_tokens(UNITS - 1)
        for m in range(4):
            products([("late", 1, m, half) for half in range(2)])
            products([("dw", 4, m, half) for half in range(2)])
        flush_stores()
